import numpy as np
import ml_dtypes


def mxq(x, axis, fmt="e4m3"):
    dtype, down = {"e4m3": (ml_dtypes.float8_e4m3fn, 7), "e5m2": (ml_dtypes.float8_e5m2, 14)}[fmt]
    v = np.moveaxis(np.asarray(x, np.float32).astype(ml_dtypes.bfloat16).astype(np.float64), axis, -1)
    blocks = v.reshape(v.shape[:-1] + (-1, 32))
    amax = np.abs(blocks).max(-1, keepdims=True)
    byte = np.maximum(np.where(amax > 0, np.frexp(amax)[1] - 1 + 127, 0) - down, 1)
    scale = np.exp2(byte - 127.0)
    codes = (blocks / scale).astype(np.float32).astype(dtype).astype(np.float64)
    return np.moveaxis((codes * scale).reshape(v.shape), -1, axis)


WIDE = False


def mx_kscale(k):
    if not WIDE:
        return np.ones(k)
    levels = np.array([10, -10, 5, -5, 0])
    a = np.random.permutation(np.resize(levels, k // 512 * 4)).reshape(k // 512, 4)
    idx = np.arange(k)
    return np.exp2(a[idx // 512, idx % 128 // 32])


BF16 = ml_dtypes.bfloat16


def bf(x):
    return np.asarray(x, np.float32).astype(BF16)


def f64(x):
    return np.asarray(x).astype(np.float64)


B, O, I, LQ, LS, D = 16, 4, 16, 32, 32, 64
FS = LS * D
KV = I * LS
EPS = 1e-5
SHIFT = 14.0


def setup_inputs():
    s = mx_kscale(FS)
    enc = np.random.standard_normal((B, I, FS)) * s
    return {
        "scores": bf(-SHIFT + 1.5 * np.random.standard_normal((B, O, I, LQ, LS))),
        "final_encoder_out": bf(enc.reshape(B, I * LS, D)),
        "WV_w": bf(np.random.standard_normal((O, FS, FS)) * 1.5 / np.sqrt(FS) / s),
        "WV_b": bf(np.random.standard_normal((O, FS)) * 0.2),
    }


def reference(scores, final_encoder_out, WV_w, WV_b):
    encq = mxq(f64(final_encoder_out).reshape(B * I, FS), 1, "e4m3")
    wq = mxq(f64(WV_w).reshape(O * FS, FS), 1, "e4m3")
    v = (encq @ wq.T) + f64(WV_b).reshape(O * FS)
    v = np.swapaxes(v.reshape(B, I, O, LS, D), 1, 2).reshape(B, O, KV, D)
    e = np.exp(f64(scores))
    attn = e / (e.sum(-1, keepdims=True) + EPS)
    attn = np.swapaxes(attn, 2, 3).reshape(B, O, LQ, KV)
    z = mxq(attn, 3, "e4m3") @ mxq(v, 2, "e4m3")
    coeff = 1.0 / np.sqrt(D)
    return (coeff * z).reshape(B, O * LQ, D)

@@ -1,0 +1,304 @@
+from contextlib import ExitStack
+
+import concourse.mybir as mybir
+from concourse.masks import make_identity
+
+BF16 = mybir.dt.bfloat16
+F32 = mybir.dt.float32
+U32 = mybir.dt.uint32
+U8 = mybir.dt.uint8
+FP8X4 = mybir.dt.float8_e4m3fn_x4
+ACT = mybir.ActivationFunctionType
+ALU = mybir.AluOpType
+AXIS = mybir.AxisListType
+
+P = 128
+B, O, I, LQ, LS, D = 16, 4, 16, 32, 32, 64
+FS = LS * D
+EPS = 1e-5
+COEFF = 0.125
+PASSES = FS // 512
+ROWS = B * I
+N_GROUPS = O * FS // (2 * P)
+HEAD_GROUPS = N_GROUPS // O
+W_AHEAD = 4
+A_FIRST = 6
+A_CHUNKS = 8
+
+FLOPS = 2 * ROWS * O * FS * FS + 2 * B * O * LQ * I * LS * D
+
+
+def tile_localcrossattention_pa_kernel(tc, scores, final_encoder_out, WV_w, WV_b, out):
+    nc = tc.nc
+
+    w_groups = WV_w.rearrange("o (g j w) f -> (o g) j w f", j=P, w=2)
+    enc_rows = final_encoder_out.rearrange("b (i s) d -> (b i) (s d)", i=I).rearrange(
+        "(h r) f -> r h f", h=2
+    )
+    score_rows = scores.rearrange("(y b) o i (h l) k -> y h (b o) i (l k)", y=2, h=4)
+    bias_rows = WV_b.rearrange("o (g x) -> (o g) x", x=2 * P)
+    out_rows = out.rearrange("(g b) (o q) d -> o b q g d", b=4, o=O)
+
+    with ExitStack() as ctx:
+        const = ctx.enter_context(tc.tile_pool(name="const", bufs=1))
+        w_in = ctx.enter_context(tc.tile_pool(name="w_in", bufs=W_AHEAD + 2))
+        w_mx = ctx.enter_context(tc.tile_pool(name="w_mx", bufs=3))
+        work = ctx.enter_context(tc.tile_pool(name="work", bufs=2))
+        ps_w = ctx.enter_context(tc.psum_pool(name="ps_w", bufs=4))
+        ps_x = ctx.enter_context(tc.psum_pool(name="ps_x", bufs=2))
+        ps_acc = ctx.enter_context(tc.psum_pool(name="ps_acc", bufs=2))
+
+        ident_f32 = const.tile([P, P], F32)
+        make_identity(nc, ident_f32[:])
+        ident_bf = const.tile([P, P], BF16)
+        make_identity(nc, ident_bf[:])
+        perm_v = const.tile([P, P], BF16)
+        nc.vector.tensor_copy(
+            out=perm_v[:].rearrange("p (c t) -> p c t", t=4),
+            in_=ident_bf[:].rearrange("p (t c) -> p c t", t=4),
+        )
+        perm_a = const.tile([P, P], BF16)
+        nc.vector.tensor_copy(
+            out=perm_a[:].rearrange("p (o b h) -> p o b h", o=O, b=8),
+            in_=ident_bf[:].rearrange("p (b o h) -> p o b h", b=8, o=O),
+        )
+
+        enc_codes = const.tile([P, PASSES, ROWS], U32, align_bytes=64)
+        enc_scales = const.tile([P, PASSES, ROWS], U8, align_bytes=64)
+        bias_sb = const.tile([P, N_GROUPS, 2], F32)
+        s_raw = const.tile([P, 2, I, 8 * LS], BF16)
+        a_grp = const.tile([P, 2, 32, 4, 4, 8], BF16, align_bytes=64)
+        a_codes = const.tile([P, 2, 32, LQ], U32, align_bytes=64)
+        a_scales = const.tile([P, 2, 32, LQ], U8, align_bytes=64)
+        v_codes = const.tile([P, O, B, D], U32, align_bytes=64)
+        v_scales = const.tile([P, O, B, D], U8, align_bytes=64)
+        o_sb = const.tile([P, O, 4, D], F32)
+
+        def copy_out(engine_is_scalar, dst, src):
+            if engine_is_scalar:
+                nc.scalar.copy(out=dst, in_=src)
+            else:
+                nc.vector.tensor_copy(out=dst, in_=src)
+
+        def transpose_two_passes(words, first_pass, grouped_words, engine_is_scalar):
+            bank = ps_w.tile([P, 2, 2, P], F32, name="bank", tag="bank")
+            for c in range(2):
+                for u in range(2):
+                    blk = 2 * (first_pass + c) + u
+                    nc.tensor.transpose(bank[:, c, u, :], words[:, blk * P : (blk + 1) * P], ident_f32[:])
+            copy_out(engine_is_scalar, grouped_words, bank[:].rearrange("p c u n -> p c n u"))
+
+        def load_w(g):
+            w_raw = w_in.tile([P, 2, FS], BF16, name="w_raw")
+            nc.sync.dma_start(out=w_raw[:], in_=w_groups[g])
+            return w_raw
+
+        def load_scores(s):
+            y, h = divmod(s, 4)
+            nc.sync.dma_start(out=s_raw[h:P:4, y], in_=score_rows[y, h])
+
+        def transpose_w(w_raw):
+            w_grp = w_mx.tile([P, 2, PASSES, P, 4], BF16, name="w_grp", align_bytes=64)
+            raw_words = w_raw[:].bitcast(F32)
+            grp_words = w_grp[:].bitcast(F32)
+            for w in range(2):
+                for half in range(2):
+                    transpose_two_passes(
+                        raw_words[:, w, :],
+                        2 * half,
+                        grp_words[:, w, 2 * half : 2 * half + 2, :, :],
+                        engine_is_scalar=(2 * w + half < 3),
+                    )
+            return w_grp
+
+        def quantise_w(w_grp):
+            w_codes = w_mx.tile([P, 2, PASSES, P], U32, name="w_codes", align_bytes=64)
+            w_scales = w_mx.tile([P, 2, PASSES, P], U8, name="w_scales", align_bytes=64)
+            nc.vector.quantize_mx(
+                out=w_codes[:].rearrange("p w c n -> p (w c n)").bitcast(FP8X4),
+                scales=w_scales[:].rearrange("p w c n -> p (w c n)"),
+                in_=w_grp[:].rearrange("p w c n t -> p (w c n t)"),
+            )
+            return w_codes, w_scales
+
+        def project(g, w_codes, w_scales, vt):
+            acc = ps_acc.tile([P, 2, ROWS], F32, name="acc", tag="acc")
+            for w in range(2):
+                for c in range(PASSES):
+                    nc.tensor.matmul_mx(
+                        out=acc[:, w, :],
+                        lhsT=w_codes[:, w, c, :].bitcast(FP8X4),
+                        lhsT_scale=w_scales[:, w, c, :],
+                        rhs=enc_codes[:, c, :].bitcast(FP8X4),
+                        rhs_scale=enc_scales[:, c, :],
+                        start=(c == 0),
+                        stop=(c == PASSES - 1),
+                    )
+            kap = g % HEAD_GROUPS
+            for w in range(2):
+                src = acc[:, w, :].rearrange("p (b i) -> p b i", i=I)
+                dst = vt[:, w, :, kap, :]
+                if g % 2 == 0:
+                    nc.scalar.activation(out=dst, in_=src, func=ACT.Identity, bias=bias_sb[:, g, w : w + 1], scale=1.0)
+                else:
+                    nc.vector.tensor_scalar(out=dst, in0=src, scalar1=bias_sb[:, g, w : w + 1], scalar2=None, op0=ALU.add)
+
+        def values_quarter(o, qd, vt):
+            bank = ps_x.tile([P, 4, 2, P], BF16, name="v_bank", tag="x")
+            for b4 in range(4):
+                for w in range(2):
+                    nc.tensor.transpose(
+                        bank[:, b4, w, :],
+                        vt[:, w, 4 * qd + b4].rearrange("p k i -> p (k i)"),
+                        perm_v[:],
+                    )
+            v_grp = work.tile([P, 4, 2, P], BF16, name="v_grp", align_bytes=64)
+            copy_out(qd % 2 == 0, v_grp[:], bank[:])
+            nc.vector.quantize_mx(
+                out=v_codes[:, o, 4 * qd : 4 * qd + 4, :].rearrange("p b n -> p (b n)").bitcast(FP8X4),
+                scales=v_scales[:, o, 4 * qd : 4 * qd + 4, :].rearrange("p b n -> p (b n)"),
+                in_=v_grp[:].rearrange("p b w n -> p (b w n)"),
+            )
+
+        def attn_exp(c):
+            y, qp = divmod(c, 4)
+            e_t = work.tile([P, I, 2 * LS], F32, name="e_t")
+            nc.scalar.activation(out=e_t[:], in_=s_raw[:, y, :, 64 * qp : 64 * qp + 64], func=ACT.Exp)
+            return e_t
+
+        def attn_normalise(e_t):
+            ssum = work.tile([P, I, 2], F32, name="ssum")
+            nc.vector.tensor_reduce(
+                out=ssum[:], in_=e_t[:].rearrange("p i (l k) -> p i l k", k=LS), axis=AXIS.X, op=ALU.add
+            )
+            nc.vector.tensor_scalar_add(out=ssum[:], in0=ssum[:], scalar1=EPS)
+            rec = work.tile([P, I, 2], F32, name="rec")
+            nc.vector.reciprocal(out=rec[:], in_=ssum[:])
+            a_n = work.tile([P, 4, 2, 8, I], BF16, name="a_n")
+            for l in range(2):
+                nc.vector.tensor_tensor(
+                    out=a_n[:, :, l].rearrange("p t k i -> p k i t"),
+                    in0=e_t[:, :, LS * l : LS * (l + 1)].rearrange("p i (k t) -> p k i t", t=4),
+                    in1=rec[:, :, l].unsqueeze(1).unsqueeze(3).to_broadcast([P, 8, I, 4]),
+                    op=ALU.mult,
+                )
+            return a_n
+
+        def attn_transpose(c, a_n):
+            y, qp = divmod(c, 4)
+            bank = ps_x.tile([P, 8, P], BF16, name="a_bank", tag="x")
+            for l in range(2):
+                for t in range(4):
+                    nc.tensor.transpose(
+                        bank[:, 4 * l + t, :], a_n[:, t, l].rearrange("p k i -> p (k i)"), perm_a[:]
+                    )
+            nc.scalar.copy(out=a_grp[:, y, :, :, qp, :], in_=bank[:].rearrange("p s (x h) -> p x h s", h=4))
+            if qp == 3:
+                nc.vector.quantize_mx(
+                    out=a_codes[:, y].rearrange("p x q -> p (x q)").bitcast(FP8X4),
+                    scales=a_scales[:, y].rearrange("p x q -> p (x q)"),
+                    in_=a_grp[:, y].rearrange("p x h g s -> p (x h g s)"),
+                )
+
+        def finish(o, qd):
+            y, gl = divmod(qd, 2)
+            x0 = 8 * o + 4 * gl
+            res = ps_acc.tile([P, 4, 2, 32], F32, name="res", tag="acc")
+            nc.tensor.matmul_mx(
+                out=res[:].rearrange("p b w c -> p (b w c)"),
+                lhsT=a_codes[:, y, x0 : x0 + 4, :].rearrange("p x q -> p (x q)").bitcast(FP8X4),
+                lhsT_scale=a_scales[:, y, x0 : x0 + 4, :].rearrange("p x q -> p (x q)"),
+                rhs=v_codes[:, o, 4 * qd : 4 * qd + 4, :].rearrange("p b n -> p (b n)").bitcast(FP8X4),
+                rhs_scale=v_scales[:, o, 4 * qd : 4 * qd + 4, :].rearrange("p b n -> p (b n)"),
+                start=True,
+                stop=True,
+            )
+            for b4 in range(4):
+                rows = slice(32 * b4, 32 * b4 + 32)
+                nc.vector.tensor_scalar(
+                    out=o_sb[rows, o, qd, :].rearrange("p (c w) -> p c w", w=2),
+                    in0=res[rows, b4].rearrange("p w c -> p c w"),
+                    scalar1=COEFF,
+                    scalar2=None,
+                    op0=ALU.mult,
+                )
+            if qd == 3:
+                for b4 in range(4):
+                    nc.sync.dma_start(out=out_rows[o, b4], in_=o_sb[32 * b4 : 32 * b4 + 32, o])
+
+        w_raw = {}
+        w_grp = {}
+        w_quant = {}
+        vt = {}
+        e_tiles = {}
+        a_tiles = {}
+        w_raw[0] = load_w(0)
+        w_raw[1] = load_w(1)
+        enc_raw = const.tile([P, 2, FS], BF16)
+        nc.sync.dma_start(out=enc_raw[:], in_=enc_rows)
+        bias_raw = const.tile([P, 2 * P], BF16)
+        nc.vector.memset(bias_raw[:], 0.0)
+        nc.sync.dma_start(out=bias_raw[0:N_GROUPS, :], in_=bias_rows)
+        w_raw[2] = load_w(2)
+        load_scores(0)
+        w_raw[3] = load_w(3)
+        load_scores(1)
+
+        def prepare_enc_and_bias():
+            enc_grp = const.tile([P, PASSES, ROWS, 4], BF16, align_bytes=64)
+            raw_words = enc_raw[:].bitcast(F32)
+            grp_words = enc_grp[:].bitcast(F32)
+            for h in range(2):
+                for half in range(2):
+                    transpose_two_passes(
+                        raw_words[:, h, :],
+                        2 * half,
+                        grp_words[:, 2 * half : 2 * half + 2, P * h : P * (h + 1), :],
+                        engine_is_scalar=(half == 0),
+                    )
+            nc.vector.quantize_mx(
+                out=enc_codes[:].rearrange("p c r -> p (c r)").bitcast(FP8X4),
+                scales=enc_scales[:].rearrange("p c r -> p (c r)"),
+                in_=enc_grp[:].rearrange("p c r t -> p (c r t)"),
+            )
+            bias_bank = ps_x.tile([P, P], F32, name="bias_bank", tag="x")
+            nc.tensor.transpose(bias_bank[:], bias_raw[:].bitcast(F32), ident_f32[:])
+            nc.vector.tensor_copy(
+                out=bias_sb[:],
+                in_=bias_bank[:].bitcast(BF16).rearrange("p (g w) -> p g w", w=2)[:, 0:N_GROUPS, :],
+            )
+
+        for p in range(N_GROUPS + 6):
+            if p + W_AHEAD < N_GROUPS:
+                w_raw[p + W_AHEAD] = load_w(p + W_AHEAD)
+            if p + 2 < 8:
+                load_scores(p + 2)
+
+            if p < N_GROUPS:
+                w_grp[p] = transpose_w(w_raw[p])
+            if p == 0:
+                prepare_enc_and_bias()
+            c, phase = divmod(p - A_FIRST, 2)
+            if phase == 0 and 1 <= c <= A_CHUNKS:
+                attn_transpose(c - 1, a_tiles[c - 1])
+            o, qd = divmod(p - HEAD_GROUPS - 1, HEAD_GROUPS)
+            if 0 <= o < O and qd < 4:
+                values_quarter(o, qd, vt[o])
+
+            if p < N_GROUPS:
+                w_quant[p] = quantise_w(w_grp[p])
+            if 1 <= p <= N_GROUPS:
+                g = p - 1
+                if g % HEAD_GROUPS == 0:
+                    vt_new = work.tile([P, 2, B, HEAD_GROUPS, I], BF16, name="vt")
+                    vt[g // HEAD_GROUPS] = vt_new
+                project(g, w_quant[g][0], w_quant[g][1], vt[g // HEAD_GROUPS])
+            for o in range(O):
+                qd = p - (HEAD_GROUPS * max(o, 2) + 10)
+                if 0 <= qd < 4:
+                    finish(o, qd)
+
+            if phase == 0 and 0 <= c < A_CHUNKS:
+                e_tiles[c] = attn_exp(c)
+            if phase == 1 and 0 <= c < A_CHUNKS:
+                a_tiles[c] = attn_normalise(e_tiles[c])

@@ -48,6 +48,8 @@ def tile_localcrossattention_pa_kernel(tc, scores, final_encoder_out, WV_w, WV_b
         ps_x = ctx.enter_context(tc.psum_pool(name="ps_x", bufs=2))
         ps_acc = ctx.enter_context(tc.psum_pool(name="ps_acc", bufs=2))
 
+        ctx.enter_context(tc.manual_schedule())
+
         ident_f32 = const.tile([P, P], F32)
         make_identity(nc, ident_f32[:])
         ident_bf = const.tile([P, P], BF16)
@@ -74,19 +76,16 @@ def tile_localcrossattention_pa_kernel(tc, scores, final_encoder_out, WV_w, WV_b
         v_scales = const.tile([P, O, B, D], U8, align_bytes=64)
         o_sb = const.tile([P, O, 4, D], F32)
 
-        def copy_out(engine_is_scalar, dst, src):
-            if engine_is_scalar:
-                nc.scalar.copy(out=dst, in_=src)
-            else:
-                nc.vector.tensor_copy(out=dst, in_=src)
-
-        def transpose_two_passes(words, first_pass, grouped_words, engine_is_scalar):
+        def transpose_two_passes(words, first_pass, grouped_words, on_scalar):
             bank = ps_w.tile([P, 2, 2, P], F32, name="bank", tag="bank")
             for c in range(2):
                 for u in range(2):
                     blk = 2 * (first_pass + c) + u
                     nc.tensor.transpose(bank[:, c, u, :], words[:, blk * P : (blk + 1) * P], ident_f32[:])
-            copy_out(engine_is_scalar, grouped_words, bank[:].rearrange("p c u n -> p c n u"))
+            if on_scalar:
+                nc.scalar.copy(out=grouped_words, in_=bank[:].rearrange("p c u n -> p c n u"))
+            else:
+                nc.vector.tensor_copy(out=grouped_words, in_=bank[:].rearrange("p c u n -> p c n u"))
 
         def load_w(g):
             w_raw = w_in.tile([P, 2, FS], BF16, name="w_raw")
@@ -107,7 +106,7 @@ def tile_localcrossattention_pa_kernel(tc, scores, final_encoder_out, WV_w, WV_b
                         raw_words[:, w, :],
                         2 * half,
                         grp_words[:, w, 2 * half : 2 * half + 2, :, :],
-                        engine_is_scalar=(2 * w + half < 3),
+                        on_scalar=(2 * w + half < 3),
                     )
             return w_grp
 
@@ -134,14 +133,14 @@ def tile_localcrossattention_pa_kernel(tc, scores, final_encoder_out, WV_w, WV_b
                         start=(c == 0),
                         stop=(c == PASSES - 1),
                     )
-            kap = g % HEAD_GROUPS
             for w in range(2):
-                src = acc[:, w, :].rearrange("p (b i) -> p b i", i=I)
-                dst = vt[:, w, :, kap, :]
-                if g % 2 == 0:
-                    nc.scalar.activation(out=dst, in_=src, func=ACT.Identity, bias=bias_sb[:, g, w : w + 1], scale=1.0)
-                else:
-                    nc.vector.tensor_scalar(out=dst, in0=src, scalar1=bias_sb[:, g, w : w + 1], scalar2=None, op0=ALU.add)
+                nc.scalar.activation(
+                    out=vt[:, w, :, g % HEAD_GROUPS, :],
+                    in_=acc[:, w, :].rearrange("p (b i) -> p b i", i=I),
+                    func=ACT.Identity,
+                    bias=bias_sb[:, g, w : w + 1],
+                    scale=1.0,
+                )
 
         def values_quarter(o, qd, vt):
             bank = ps_x.tile([P, 4, 2, P], BF16, name="v_bank", tag="x")
@@ -153,7 +152,10 @@ def tile_localcrossattention_pa_kernel(tc, scores, final_encoder_out, WV_w, WV_b
                         perm_v[:],
                     )
             v_grp = work.tile([P, 4, 2, P], BF16, name="v_grp", align_bytes=64)
-            copy_out(qd % 2 == 0, v_grp[:], bank[:])
+            nc.vector.tensor_copy(out=v_grp[:], in_=bank[:])
+            return v_grp
+
+        def quantise_values(o, qd, v_grp):
             nc.vector.quantize_mx(
                 out=v_codes[:, o, 4 * qd : 4 * qd + 4, :].rearrange("p b n -> p (b n)").bitcast(FP8X4),
                 scales=v_scales[:, o, 4 * qd : 4 * qd + 4, :].rearrange("p b n -> p (b n)"),
@@ -166,7 +168,7 @@ def tile_localcrossattention_pa_kernel(tc, scores, final_encoder_out, WV_w, WV_b
             nc.scalar.activation(out=e_t[:], in_=s_raw[:, y, :, 64 * qp : 64 * qp + 64], func=ACT.Exp)
             return e_t
 
-        def attn_normalise(e_t):
+        def attn_reciprocal(e_t):
             ssum = work.tile([P, I, 2], F32, name="ssum")
             nc.vector.tensor_reduce(
                 out=ssum[:], in_=e_t[:].rearrange("p i (l k) -> p i l k", k=LS), axis=AXIS.X, op=ALU.add
@@ -174,6 +176,9 @@ def tile_localcrossattention_pa_kernel(tc, scores, final_encoder_out, WV_w, WV_b
             nc.vector.tensor_scalar_add(out=ssum[:], in0=ssum[:], scalar1=EPS)
             rec = work.tile([P, I, 2], F32, name="rec")
             nc.vector.reciprocal(out=rec[:], in_=ssum[:])
+            return rec
+
+        def attn_scale(e_t, rec):
             a_n = work.tile([P, 4, 2, 8, I], BF16, name="a_n")
             for l in range(2):
                 nc.vector.tensor_tensor(
@@ -193,36 +198,37 @@ def tile_localcrossattention_pa_kernel(tc, scores, final_encoder_out, WV_w, WV_b
                         bank[:, 4 * l + t, :], a_n[:, t, l].rearrange("p k i -> p (k i)"), perm_a[:]
                     )
             nc.scalar.copy(out=a_grp[:, y, :, :, qp, :], in_=bank[:].rearrange("p s (x h) -> p x h s", h=4))
-            if qp == 3:
-                nc.vector.quantize_mx(
-                    out=a_codes[:, y].rearrange("p x q -> p (x q)").bitcast(FP8X4),
-                    scales=a_scales[:, y].rearrange("p x q -> p (x q)"),
-                    in_=a_grp[:, y].rearrange("p x h g s -> p (x h g s)"),
-                )
 
-        def finish(o, qd):
-            y, gl = divmod(qd, 2)
-            x0 = 8 * o + 4 * gl
-            res = ps_acc.tile([P, 4, 2, 32], F32, name="res", tag="acc")
-            nc.tensor.matmul_mx(
-                out=res[:].rearrange("p b w c -> p (b w c)"),
-                lhsT=a_codes[:, y, x0 : x0 + 4, :].rearrange("p x q -> p (x q)").bitcast(FP8X4),
-                lhsT_scale=a_scales[:, y, x0 : x0 + 4, :].rearrange("p x q -> p (x q)"),
-                rhs=v_codes[:, o, 4 * qd : 4 * qd + 4, :].rearrange("p b n -> p (b n)").bitcast(FP8X4),
-                rhs_scale=v_scales[:, o, 4 * qd : 4 * qd + 4, :].rearrange("p b n -> p (b n)"),
-                start=True,
-                stop=True,
+        def quantise_attn(y):
+            nc.vector.quantize_mx(
+                out=a_codes[:, y].rearrange("p x q -> p (x q)").bitcast(FP8X4),
+                scales=a_scales[:, y].rearrange("p x q -> p (x q)"),
+                in_=a_grp[:, y].rearrange("p x h g s -> p (x h g s)"),
             )
+
+        def finish(o, y):
+            res = ps_acc.tile([P, 2, 4, 2, 32], F32, name="res", tag="acc")
+            for gl in range(2):
+                x0 = 8 * o + 4 * gl
+                b0 = 8 * y + 4 * gl
+                nc.tensor.matmul_mx(
+                    out=res[:, gl].rearrange("p b w c -> p (b w c)"),
+                    lhsT=a_codes[:, y, x0 : x0 + 4, :].rearrange("p x q -> p (x q)").bitcast(FP8X4),
+                    lhsT_scale=a_scales[:, y, x0 : x0 + 4, :].rearrange("p x q -> p (x q)"),
+                    rhs=v_codes[:, o, b0 : b0 + 4, :].rearrange("p b n -> p (b n)").bitcast(FP8X4),
+                    rhs_scale=v_scales[:, o, b0 : b0 + 4, :].rearrange("p b n -> p (b n)"),
+                    start=True,
+                    stop=True,
+                )
             for b4 in range(4):
                 rows = slice(32 * b4, 32 * b4 + 32)
-                nc.vector.tensor_scalar(
-                    out=o_sb[rows, o, qd, :].rearrange("p (c w) -> p c w", w=2),
-                    in0=res[rows, b4].rearrange("p w c -> p c w"),
-                    scalar1=COEFF,
-                    scalar2=None,
-                    op0=ALU.mult,
-                )
-            if qd == 3:
+                dst = o_sb[rows, o, 2 * y : 2 * y + 2, :].rearrange("p g (c w) -> p g c w", w=2)
+                src = res[rows, :, b4].rearrange("p g w c -> p g c w")
+                if y == 0:
+                    nc.scalar.mul(out=dst, in_=src, mul=COEFF)
+                else:
+                    nc.vector.tensor_scalar(out=dst, in0=src, scalar1=COEFF, scalar2=None, op0=ALU.mult)
+            if y == 1:
                 for b4 in range(4):
                     nc.sync.dma_start(out=out_rows[o, b4], in_=o_sb[32 * b4 : 32 * b4 + 32, o])
 
@@ -231,14 +237,15 @@ def tile_localcrossattention_pa_kernel(tc, scores, final_encoder_out, WV_w, WV_b
         w_quant = {}
         vt = {}
         e_tiles = {}
+        rec_tiles = {}
         a_tiles = {}
         w_raw[0] = load_w(0)
-        w_raw[1] = load_w(1)
         enc_raw = const.tile([P, 2, FS], BF16)
         nc.sync.dma_start(out=enc_raw[:], in_=enc_rows)
         bias_raw = const.tile([P, 2 * P], BF16)
         nc.vector.memset(bias_raw[:], 0.0)
         nc.sync.dma_start(out=bias_raw[0:N_GROUPS, :], in_=bias_rows)
+        w_raw[1] = load_w(1)
         w_raw[2] = load_w(2)
         load_scores(0)
         w_raw[3] = load_w(3)
@@ -254,18 +261,18 @@ def tile_localcrossattention_pa_kernel(tc, scores, final_encoder_out, WV_w, WV_b
                         raw_words[:, h, :],
                         2 * half,
                         grp_words[:, 2 * half : 2 * half + 2, P * h : P * (h + 1), :],
-                        engine_is_scalar=(half == 0),
+                        on_scalar=(half == 0),
                     )
-            nc.vector.quantize_mx(
-                out=enc_codes[:].rearrange("p c r -> p (c r)").bitcast(FP8X4),
-                scales=enc_scales[:].rearrange("p c r -> p (c r)"),
-                in_=enc_grp[:].rearrange("p c r t -> p (c r t)"),
-            )
             bias_bank = ps_x.tile([P, P], F32, name="bias_bank", tag="x")
             nc.tensor.transpose(bias_bank[:], bias_raw[:].bitcast(F32), ident_f32[:])
             nc.vector.tensor_copy(
                 out=bias_sb[:],
                 in_=bias_bank[:].bitcast(BF16).rearrange("p (g w) -> p g w", w=2)[:, 0:N_GROUPS, :],
+            )
+            nc.vector.quantize_mx(
+                out=enc_codes[:].rearrange("p c r -> p (c r)").bitcast(FP8X4),
+                scales=enc_scales[:].rearrange("p c r -> p (c r)"),
+                in_=enc_grp[:].rearrange("p c r t -> p (c r t)"),
             )
 
         for p in range(N_GROUPS + 6):
@@ -278,15 +285,30 @@ def tile_localcrossattention_pa_kernel(tc, scores, final_encoder_out, WV_w, WV_b
                 w_grp[p] = transpose_w(w_raw[p])
             if p == 0:
                 prepare_enc_and_bias()
-            c, phase = divmod(p - A_FIRST, 2)
-            if phase == 0 and 1 <= c <= A_CHUNKS:
+            c, phase = divmod(p - A_FIRST, 3)
+            if phase == 1 and 1 <= c <= A_CHUNKS:
                 attn_transpose(c - 1, a_tiles[c - 1])
             o, qd = divmod(p - HEAD_GROUPS - 1, HEAD_GROUPS)
-            if 0 <= o < O and qd < 4:
-                values_quarter(o, qd, vt[o])
+            v_now = 0 <= o < O and qd < 4
+            if v_now:
+                v_grp = values_quarter(o, qd, vt[o])
 
+            if 0 <= c < A_CHUNKS:
+                if phase == 0:
+                    e_tiles[c] = attn_exp(c)
+                if phase == 1:
+                    rec_tiles[c] = attn_reciprocal(e_tiles[c])
+                if phase == 2:
+                    a_tiles[c] = attn_scale(e_tiles[c], rec_tiles[c])
+            for y in range(2):
+                if p == A_FIRST + 12 * y + 14:
+                    quantise_attn(y)
+
+            if v_now:
+                quantise_values(o, qd, v_grp)
             if p < N_GROUPS:
                 w_quant[p] = quantise_w(w_grp[p])
+
             if 1 <= p <= N_GROUPS:
                 g = p - 1
                 if g % HEAD_GROUPS == 0:
@@ -294,11 +316,6 @@ def tile_localcrossattention_pa_kernel(tc, scores, final_encoder_out, WV_w, WV_b
                     vt[g // HEAD_GROUPS] = vt_new
                 project(g, w_quant[g][0], w_quant[g][1], vt[g // HEAD_GROUPS])
             for o in range(O):
-                qd = p - (HEAD_GROUPS * max(o, 2) + 10)
-                if 0 <= qd < 4:
-                    finish(o, qd)
-
-            if phase == 0 and 0 <= c < A_CHUNKS:
-                e_tiles[c] = attn_exp(c)
-            if phase == 1 and 0 <= c < A_CHUNKS:
-                a_tiles[c] = attn_normalise(e_tiles[c])
+                for y in range(2):
+                    if p == max(HEAD_GROUPS * o + 11 + 2 * y, A_FIRST + 12 * y + 15):
+                        finish(o, y)

@@ -21,9 +21,12 @@ PASSES = FS // 512
 ROWS = B * I
 N_GROUPS = O * FS // (2 * P)
 HEAD_GROUPS = N_GROUPS // O
+N_UNITS = 2 * N_GROUPS
+HEAD_UNITS = N_UNITS // O
 W_AHEAD = 4
-A_FIRST = 6
+A_FIRST = 13
 A_CHUNKS = 8
+A_PERIODS = 6
 
 FLOPS = 2 * ROWS * O * FS * FS + 2 * B * O * LQ * I * LS * D
 
@@ -42,7 +45,7 @@ def tile_localcrossattention_pa_kernel(tc, scores, final_encoder_out, WV_w, WV_b
     with ExitStack() as ctx:
         const = ctx.enter_context(tc.tile_pool(name="const", bufs=1))
         w_in = ctx.enter_context(tc.tile_pool(name="w_in", bufs=W_AHEAD + 2))
-        w_mx = ctx.enter_context(tc.tile_pool(name="w_mx", bufs=3))
+        w_mx = ctx.enter_context(tc.tile_pool(name="w_mx", bufs=4))
         work = ctx.enter_context(tc.tile_pool(name="work", bufs=2))
         ps_w = ctx.enter_context(tc.psum_pool(name="ps_w", bufs=4))
         ps_x = ctx.enter_context(tc.psum_pool(name="ps_x", bufs=2))
@@ -96,51 +99,48 @@ def tile_localcrossattention_pa_kernel(tc, scores, final_encoder_out, WV_w, WV_b
             y, h = divmod(s, 4)
             nc.sync.dma_start(out=s_raw[h:P:4, y], in_=score_rows[y, h])
 
-        def transpose_w(w_raw):
-            w_grp = w_mx.tile([P, 2, PASSES, P, 4], BF16, name="w_grp", align_bytes=64)
+        def transpose_w(w_raw, w):
+            w_grp = w_mx.tile([P, PASSES, P, 4], BF16, name="w_grp", align_bytes=64)
             raw_words = w_raw[:].bitcast(F32)
             grp_words = w_grp[:].bitcast(F32)
-            for w in range(2):
-                for half in range(2):
-                    transpose_two_passes(
-                        raw_words[:, w, :],
-                        2 * half,
-                        grp_words[:, w, 2 * half : 2 * half + 2, :, :],
-                        on_scalar=(2 * w + half < 3),
-                    )
+            for half in range(2):
+                transpose_two_passes(
+                    raw_words[:, w, :],
+                    2 * half,
+                    grp_words[:, 2 * half : 2 * half + 2, :, :],
+                    on_scalar=(2 * w + half < 3),
+                )
             return w_grp
 
         def quantise_w(w_grp):
-            w_codes = w_mx.tile([P, 2, PASSES, P], U32, name="w_codes", align_bytes=64)
-            w_scales = w_mx.tile([P, 2, PASSES, P], U8, name="w_scales", align_bytes=64)
+            w_codes = w_mx.tile([P, PASSES, P], U32, name="w_codes", align_bytes=64)
+            w_scales = w_mx.tile([P, PASSES, P], U8, name="w_scales", align_bytes=64)
             nc.vector.quantize_mx(
-                out=w_codes[:].rearrange("p w c n -> p (w c n)").bitcast(FP8X4),
-                scales=w_scales[:].rearrange("p w c n -> p (w c n)"),
-                in_=w_grp[:].rearrange("p w c n t -> p (w c n t)"),
+                out=w_codes[:].rearrange("p c n -> p (c n)").bitcast(FP8X4),
+                scales=w_scales[:].rearrange("p c n -> p (c n)"),
+                in_=w_grp[:].rearrange("p c n t -> p (c n t)"),
             )
             return w_codes, w_scales
 
-        def project(g, w_codes, w_scales, vt):
-            acc = ps_acc.tile([P, 2, ROWS], F32, name="acc", tag="acc")
-            for w in range(2):
-                for c in range(PASSES):
-                    nc.tensor.matmul_mx(
-                        out=acc[:, w, :],
-                        lhsT=w_codes[:, w, c, :].bitcast(FP8X4),
-                        lhsT_scale=w_scales[:, w, c, :],
-                        rhs=enc_codes[:, c, :].bitcast(FP8X4),
-                        rhs_scale=enc_scales[:, c, :],
-                        start=(c == 0),
-                        stop=(c == PASSES - 1),
-                    )
-            for w in range(2):
-                nc.scalar.activation(
-                    out=vt[:, w, :, g % HEAD_GROUPS, :],
-                    in_=acc[:, w, :].rearrange("p (b i) -> p b i", i=I),
-                    func=ACT.Identity,
-                    bias=bias_sb[:, g, w : w + 1],
-                    scale=1.0,
+        def project(g, w, w_codes, w_scales, vt):
+            acc = ps_acc.tile([P, ROWS], F32, name="acc", tag="acc")
+            for c in range(PASSES):
+                nc.tensor.matmul_mx(
+                    out=acc[:],
+                    lhsT=w_codes[:, c, :].bitcast(FP8X4),
+                    lhsT_scale=w_scales[:, c, :],
+                    rhs=enc_codes[:, c, :].bitcast(FP8X4),
+                    rhs_scale=enc_scales[:, c, :],
+                    start=(c == 0),
+                    stop=(c == PASSES - 1),
                 )
+            nc.scalar.activation(
+                out=vt[:, w, :, g % HEAD_GROUPS, :],
+                in_=acc[:].rearrange("p (b i) -> p b i", i=I),
+                func=ACT.Identity,
+                bias=bias_sb[:, g, w : w + 1],
+                scale=1.0,
+            )
 
         def values_quarter(o, qd, vt):
             bank = ps_x.tile([P, 4, 2, P], BF16, name="v_bank", tag="x")
@@ -178,16 +178,13 @@ def tile_localcrossattention_pa_kernel(tc, scores, final_encoder_out, WV_w, WV_b
             nc.vector.reciprocal(out=rec[:], in_=ssum[:])
             return rec
 
-        def attn_scale(e_t, rec):
-            a_n = work.tile([P, 4, 2, 8, I], BF16, name="a_n")
-            for l in range(2):
-                nc.vector.tensor_tensor(
-                    out=a_n[:, :, l].rearrange("p t k i -> p k i t"),
-                    in0=e_t[:, :, LS * l : LS * (l + 1)].rearrange("p i (k t) -> p k i t", t=4),
-                    in1=rec[:, :, l].unsqueeze(1).unsqueeze(3).to_broadcast([P, 8, I, 4]),
-                    op=ALU.mult,
-                )
-            return a_n
+        def attn_scale(e_t, rec, a_n, l):
+            nc.vector.tensor_tensor(
+                out=a_n[:, :, l].rearrange("p t k i -> p k i t"),
+                in0=e_t[:, :, LS * l : LS * (l + 1)].rearrange("p i (k t) -> p k i t", t=4),
+                in1=rec[:, :, l].unsqueeze(1).unsqueeze(3).to_broadcast([P, 8, I, 4]),
+                op=ALU.mult,
+            )
 
         def attn_transpose(c, a_n):
             y, qp = divmod(c, 4)
@@ -238,6 +235,7 @@ def tile_localcrossattention_pa_kernel(tc, scores, final_encoder_out, WV_w, WV_b
         vt = {}
         e_tiles = {}
         rec_tiles = {}
+        v_tiles = {}
         a_tiles = {}
         w_raw[0] = load_w(0)
         enc_raw = const.tile([P, 2, FS], BF16)
@@ -275,47 +273,53 @@ def tile_localcrossattention_pa_kernel(tc, scores, final_encoder_out, WV_w, WV_b
                 in_=enc_grp[:].rearrange("p c r t -> p (c r t)"),
             )
 
-        for p in range(N_GROUPS + 6):
-            if p + W_AHEAD < N_GROUPS:
-                w_raw[p + W_AHEAD] = load_w(p + W_AHEAD)
-            if p + 2 < 8:
-                load_scores(p + 2)
+        for p in range(N_UNITS + 11):
+            g_new, w_new = divmod(p, 2)
+            if w_new == 0:
+                if g_new + W_AHEAD < N_GROUPS:
+                    w_raw[g_new + W_AHEAD] = load_w(g_new + W_AHEAD)
+                if g_new + 2 < 8:
+                    load_scores(g_new + 2)
 
-            if p < N_GROUPS:
-                w_grp[p] = transpose_w(w_raw[p])
-            if p == 0:
+            if p < N_UNITS:
+                w_grp[p] = transpose_w(w_raw[g_new], w_new)
+            if p == 1:
                 prepare_enc_and_bias()
-            c, phase = divmod(p - A_FIRST, 3)
-            if phase == 1 and 1 <= c <= A_CHUNKS:
-                attn_transpose(c - 1, a_tiles[c - 1])
-            o, qd = divmod(p - HEAD_GROUPS - 1, HEAD_GROUPS)
-            v_now = 0 <= o < O and qd < 4
-            if v_now:
-                v_grp = values_quarter(o, qd, vt[o])
+            c, phase = divmod(p - A_FIRST, A_PERIODS)
+            chunk_now = 0 <= c < A_CHUNKS
+            if chunk_now and phase == 4:
+                attn_transpose(c, a_tiles[c])
+            o, step = divmod(p - HEAD_UNITS - 2, HEAD_UNITS)
+            v_now = 0 <= o < O and step < 8
+            if v_now and step % 2 == 0:
+                v_tiles[o, step // 2] = values_quarter(o, step // 2, vt[o])
 
-            if 0 <= c < A_CHUNKS:
+            if 1 <= p <= N_UNITS:
+                w_quant[p - 1] = quantise_w(w_grp[p - 1])
+            if v_now and step % 2 == 1:
+                quantise_values(o, step // 2, v_tiles[o, step // 2])
+
+            if 2 <= p < N_UNITS + 2:
+                g, w = divmod(p - 2, 2)
+                if (p - 2) % HEAD_UNITS == 0:
+                    vt_new = work.tile([P, 2, B, HEAD_GROUPS, I], BF16, name="vt")
+                    vt[g // HEAD_GROUPS] = vt_new
+                project(g, w, w_quant[p - 2][0], w_quant[p - 2][1], vt[g // HEAD_GROUPS])
+            for o in range(O):
+                for y in range(2):
+                    if p == max(HEAD_UNITS * o + 22 + 4 * y, A_FIRST + 24 * y + 24):
+                        finish(o, y)
+
+            if chunk_now:
                 if phase == 0:
                     e_tiles[c] = attn_exp(c)
                 if phase == 1:
                     rec_tiles[c] = attn_reciprocal(e_tiles[c])
                 if phase == 2:
-                    a_tiles[c] = attn_scale(e_tiles[c], rec_tiles[c])
-            for y in range(2):
-                if p == A_FIRST + 12 * y + 14:
-                    quantise_attn(y)
-
-            if v_now:
-                quantise_values(o, qd, v_grp)
-            if p < N_GROUPS:
-                w_quant[p] = quantise_w(w_grp[p])
-
-            if 1 <= p <= N_GROUPS:
-                g = p - 1
-                if g % HEAD_GROUPS == 0:
-                    vt_new = work.tile([P, 2, B, HEAD_GROUPS, I], BF16, name="vt")
-                    vt[g // HEAD_GROUPS] = vt_new
-                project(g, w_quant[g][0], w_quant[g][1], vt[g // HEAD_GROUPS])
-            for o in range(O):
-                for y in range(2):
-                    if p == max(HEAD_GROUPS * o + 11 + 2 * y, A_FIRST + 12 * y + 15):
-                        finish(o, y)
+                    a_new = work.tile([P, 4, 2, 8, I], BF16, name="a_n")
+                    a_tiles[c] = a_new
+                    attn_scale(e_tiles[c], rec_tiles[c], a_tiles[c], 0)
+                if phase == 3:
+                    attn_scale(e_tiles[c], rec_tiles[c], a_tiles[c], 1)
+                if phase == 5 and c % 4 == 3:
+                    quantise_attn(c // 4)

@@ -21,12 +21,12 @@ PASSES = FS // 512
 ROWS = B * I
 N_GROUPS = O * FS // (2 * P)
 HEAD_GROUPS = N_GROUPS // O
-N_UNITS = 2 * N_GROUPS
-HEAD_UNITS = N_UNITS // O
 W_AHEAD = 4
-A_FIRST = 13
+MX_LAG = 2
+A_FIRST = 3
 A_CHUNKS = 8
-A_PERIODS = 6
+A_EVERY = 3
+V_FIRST = HEAD_GROUPS + MX_LAG
 
 FLOPS = 2 * ROWS * O * FS * FS + 2 * B * O * LQ * I * LS * D
 
@@ -45,10 +45,10 @@ def tile_localcrossattention_pa_kernel(tc, scores, final_encoder_out, WV_w, WV_b
     with ExitStack() as ctx:
         const = ctx.enter_context(tc.tile_pool(name="const", bufs=1))
         w_in = ctx.enter_context(tc.tile_pool(name="w_in", bufs=W_AHEAD + 2))
-        w_mx = ctx.enter_context(tc.tile_pool(name="w_mx", bufs=4))
+        w_bf = ctx.enter_context(tc.tile_pool(name="w_bf", bufs=2))
+        w_mx = ctx.enter_context(tc.tile_pool(name="w_mx", bufs=MX_LAG + 2))
         work = ctx.enter_context(tc.tile_pool(name="work", bufs=2))
-        ps_w = ctx.enter_context(tc.psum_pool(name="ps_w", bufs=4))
-        ps_x = ctx.enter_context(tc.psum_pool(name="ps_x", bufs=2))
+        ps_t = ctx.enter_context(tc.psum_pool(name="ps_t", bufs=6))
         ps_acc = ctx.enter_context(tc.psum_pool(name="ps_acc", bufs=2))
 
         ctx.enter_context(tc.manual_schedule())
@@ -77,10 +77,10 @@ def tile_localcrossattention_pa_kernel(tc, scores, final_encoder_out, WV_w, WV_b
         a_scales = const.tile([P, 2, 32, LQ], U8, align_bytes=64)
         v_codes = const.tile([P, O, B, D], U32, align_bytes=64)
         v_scales = const.tile([P, O, B, D], U8, align_bytes=64)
-        o_sb = const.tile([P, O, 4, D], F32)
+        o_sb = const.tile([P, O, 4, 4, D], F32)
 
         def transpose_two_passes(words, first_pass, grouped_words, on_scalar):
-            bank = ps_w.tile([P, 2, 2, P], F32, name="bank", tag="bank")
+            bank = ps_t.tile([P, 2, 2, P], F32, name="bank", tag="bank")
             for c in range(2):
                 for u in range(2):
                     blk = 2 * (first_pass + c) + u
@@ -99,51 +99,54 @@ def tile_localcrossattention_pa_kernel(tc, scores, final_encoder_out, WV_w, WV_b
             y, h = divmod(s, 4)
             nc.sync.dma_start(out=s_raw[h:P:4, y], in_=score_rows[y, h])
 
-        def transpose_w(w_raw, w):
-            w_grp = w_mx.tile([P, PASSES, P, 4], BF16, name="w_grp", align_bytes=64)
+        def transpose_w(w_raw):
+            w_grp = w_bf.tile([P, 2, PASSES, P, 4], BF16, name="w_grp", align_bytes=64)
             raw_words = w_raw[:].bitcast(F32)
             grp_words = w_grp[:].bitcast(F32)
-            for half in range(2):
-                transpose_two_passes(
-                    raw_words[:, w, :],
-                    2 * half,
-                    grp_words[:, 2 * half : 2 * half + 2, :, :],
-                    on_scalar=(2 * w + half < 3),
-                )
+            for w in range(2):
+                for half in range(2):
+                    transpose_two_passes(
+                        raw_words[:, w, :],
+                        2 * half,
+                        grp_words[:, w, 2 * half : 2 * half + 2, :, :],
+                        on_scalar=(2 * w + half < 3),
+                    )
             return w_grp
 
         def quantise_w(w_grp):
-            w_codes = w_mx.tile([P, PASSES, P], U32, name="w_codes", align_bytes=64)
-            w_scales = w_mx.tile([P, PASSES, P], U8, name="w_scales", align_bytes=64)
+            w_codes = w_mx.tile([P, 2, PASSES, P], U32, name="w_codes", align_bytes=64)
+            w_scales = w_mx.tile([P, 2, PASSES, P], U8, name="w_scales", align_bytes=64)
             nc.vector.quantize_mx(
-                out=w_codes[:].rearrange("p c n -> p (c n)").bitcast(FP8X4),
-                scales=w_scales[:].rearrange("p c n -> p (c n)"),
-                in_=w_grp[:].rearrange("p c n t -> p (c n t)"),
+                out=w_codes[:].rearrange("p w c n -> p (w c n)").bitcast(FP8X4),
+                scales=w_scales[:].rearrange("p w c n -> p (w c n)"),
+                in_=w_grp[:].rearrange("p w c n t -> p (w c n t)"),
             )
             return w_codes, w_scales
 
-        def project(g, w, w_codes, w_scales, vt):
-            acc = ps_acc.tile([P, ROWS], F32, name="acc", tag="acc")
-            for c in range(PASSES):
-                nc.tensor.matmul_mx(
-                    out=acc[:],
-                    lhsT=w_codes[:, c, :].bitcast(FP8X4),
-                    lhsT_scale=w_scales[:, c, :],
-                    rhs=enc_codes[:, c, :].bitcast(FP8X4),
-                    rhs_scale=enc_scales[:, c, :],
-                    start=(c == 0),
-                    stop=(c == PASSES - 1),
+        def project(g, w_codes, w_scales, vt):
+            acc = ps_acc.tile([P, 2, ROWS], F32, name="acc", tag="acc")
+            for w in range(2):
+                for c in range(PASSES):
+                    nc.tensor.matmul_mx(
+                        out=acc[:, w, :],
+                        lhsT=w_codes[:, w, c, :].bitcast(FP8X4),
+                        lhsT_scale=w_scales[:, w, c, :],
+                        rhs=enc_codes[:, c, :].bitcast(FP8X4),
+                        rhs_scale=enc_scales[:, c, :],
+                        start=(c == 0),
+                        stop=(c == PASSES - 1),
+                    )
+            for w in range(2):
+                nc.scalar.activation(
+                    out=vt[:, w, :, g % HEAD_GROUPS, :],
+                    in_=acc[:, w, :].rearrange("p (b i) -> p b i", i=I),
+                    func=ACT.Identity,
+                    bias=bias_sb[:, g, w : w + 1],
+                    scale=1.0,
                 )
-            nc.scalar.activation(
-                out=vt[:, w, :, g % HEAD_GROUPS, :],
-                in_=acc[:].rearrange("p (b i) -> p b i", i=I),
-                func=ACT.Identity,
-                bias=bias_sb[:, g, w : w + 1],
-                scale=1.0,
-            )
 
         def values_quarter(o, qd, vt):
-            bank = ps_x.tile([P, 4, 2, P], BF16, name="v_bank", tag="x")
+            bank = ps_t.tile([P, 4, 2, P], BF16, name="v_bank", tag="bank")
             for b4 in range(4):
                 for w in range(2):
                     nc.tensor.transpose(
@@ -188,7 +191,7 @@ def tile_localcrossattention_pa_kernel(tc, scores, final_encoder_out, WV_w, WV_b
 
         def attn_transpose(c, a_n):
             y, qp = divmod(c, 4)
-            bank = ps_x.tile([P, 8, P], BF16, name="a_bank", tag="x")
+            bank = ps_t.tile([P, 8, P], BF16, name="a_bank", tag="bank")
             for l in range(2):
                 for t in range(4):
                     nc.tensor.transpose(
@@ -217,17 +220,14 @@ def tile_localcrossattention_pa_kernel(tc, scores, final_encoder_out, WV_w, WV_b
                     start=True,
                     stop=True,
                 )
-            for b4 in range(4):
-                rows = slice(32 * b4, 32 * b4 + 32)
-                dst = o_sb[rows, o, 2 * y : 2 * y + 2, :].rearrange("p g (c w) -> p g c w", w=2)
-                src = res[rows, :, b4].rearrange("p g w c -> p g c w")
-                if y == 0:
-                    nc.scalar.mul(out=dst, in_=src, mul=COEFF)
-                else:
-                    nc.vector.tensor_scalar(out=dst, in0=src, scalar1=COEFF, scalar2=None, op0=ALU.mult)
-            if y == 1:
+            dst = o_sb[:, o, 2 * y : 2 * y + 2].rearrange("p g b (c w) -> p (g b) c w", w=2)
+            src = res[:].rearrange("p g b w c -> p (g b) c w")
+            if y == 0:
+                nc.scalar.mul(out=dst, in_=src, mul=COEFF)
+            else:
+                nc.vector.tensor_scalar(out=dst, in0=src, scalar1=COEFF, scalar2=None, op0=ALU.mult)
                 for b4 in range(4):
-                    nc.sync.dma_start(out=out_rows[o, b4], in_=o_sb[32 * b4 : 32 * b4 + 32, o])
+                    nc.sync.dma_start(out=out_rows[o, b4], in_=o_sb[32 * b4 : 32 * b4 + 32, o, :, b4, :])
 
         w_raw = {}
         w_grp = {}
@@ -235,7 +235,6 @@ def tile_localcrossattention_pa_kernel(tc, scores, final_encoder_out, WV_w, WV_b
         vt = {}
         e_tiles = {}
         rec_tiles = {}
-        v_tiles = {}
         a_tiles = {}
         w_raw[0] = load_w(0)
         enc_raw = const.tile([P, 2, FS], BF16)
@@ -244,10 +243,12 @@ def tile_localcrossattention_pa_kernel(tc, scores, final_encoder_out, WV_w, WV_b
         nc.vector.memset(bias_raw[:], 0.0)
         nc.sync.dma_start(out=bias_raw[0:N_GROUPS, :], in_=bias_rows)
         w_raw[1] = load_w(1)
-        w_raw[2] = load_w(2)
         load_scores(0)
-        w_raw[3] = load_w(3)
         load_scores(1)
+        w_raw[2] = load_w(2)
+        load_scores(2)
+        load_scores(3)
+        w_raw[3] = load_w(3)
 
         def prepare_enc_and_bias():
             enc_grp = const.tile([P, PASSES, ROWS, 4], BF16, align_bytes=64)
@@ -261,7 +262,7 @@ def tile_localcrossattention_pa_kernel(tc, scores, final_encoder_out, WV_w, WV_b
                         grp_words[:, 2 * half : 2 * half + 2, P * h : P * (h + 1), :],
                         on_scalar=(half == 0),
                     )
-            bias_bank = ps_x.tile([P, P], F32, name="bias_bank", tag="x")
+            bias_bank = ps_t.tile([P, P], F32, name="bias_bank", tag="bank")
             nc.tensor.transpose(bias_bank[:], bias_raw[:].bitcast(F32), ident_f32[:])
             nc.vector.tensor_copy(
                 out=bias_sb[:],
@@ -273,53 +274,64 @@ def tile_localcrossattention_pa_kernel(tc, scores, final_encoder_out, WV_w, WV_b
                 in_=enc_grp[:].rearrange("p c r t -> p (c r t)"),
             )
 
-        for p in range(N_UNITS + 11):
-            g_new, w_new = divmod(p, 2)
-            if w_new == 0:
-                if g_new + W_AHEAD < N_GROUPS:
-                    w_raw[g_new + W_AHEAD] = load_w(g_new + W_AHEAD)
-                if g_new + 2 < 8:
-                    load_scores(g_new + 2)
+        def chunk_at(p, offset):
+            c, rest = divmod(p - A_FIRST - offset, A_EVERY)
+            return c if rest == 0 and 0 <= c < A_CHUNKS else None
 
-            if p < N_UNITS:
-                w_grp[p] = transpose_w(w_raw[g_new], w_new)
-            if p == 1:
+        def attn_ready(y):
+            return A_FIRST + A_EVERY * (4 * y + 3) + 6
+
+        def finish_period(o, y):
+            return max(HEAD_GROUPS * o + V_FIRST + 4 + y, attn_ready(y) + 1 + o)
+
+        for p in range(finish_period(O - 1, 1) + 1):
+            if 0 <= p < N_GROUPS - W_AHEAD:
+                w_raw[p + W_AHEAD] = load_w(p + W_AHEAD)
+            if 0 <= p < 4:
+                load_scores(p + 4)
+
+            if 0 <= p < N_GROUPS:
+                w_grp[p] = transpose_w(w_raw[p])
+            if p == 0:
                 prepare_enc_and_bias()
-            c, phase = divmod(p - A_FIRST, A_PERIODS)
-            chunk_now = 0 <= c < A_CHUNKS
-            if chunk_now and phase == 4:
+            c = chunk_at(p, 5)
+            if c is not None:
                 attn_transpose(c, a_tiles[c])
-            o, step = divmod(p - HEAD_UNITS - 2, HEAD_UNITS)
-            v_now = 0 <= o < O and step < 8
-            if v_now and step % 2 == 0:
-                v_tiles[o, step // 2] = values_quarter(o, step // 2, vt[o])
+            o, qd = divmod(p - V_FIRST, HEAD_GROUPS)
+            v_now = 0 <= o < O and qd < 4
+            if v_now:
+                v_grp = values_quarter(o, qd, vt[o])
 
-            if 1 <= p <= N_UNITS:
-                w_quant[p - 1] = quantise_w(w_grp[p - 1])
-            if v_now and step % 2 == 1:
-                quantise_values(o, step // 2, v_tiles[o, step // 2])
+            c = chunk_at(p, 0)
+            if c is not None:
+                e_tiles[c] = attn_exp(c)
+            c = chunk_at(p, 3)
+            if c is not None:
+                attn_scale(e_tiles[c], rec_tiles[c], a_tiles[c], 1)
+            c = chunk_at(p, 1)
+            if c is not None:
+                rec_tiles[c] = attn_reciprocal(e_tiles[c])
+            c = chunk_at(p, 2)
+            if c is not None:
+                a_new = work.tile([P, 4, 2, 8, I], BF16, name="a_n")
+                a_tiles[c] = a_new
+                attn_scale(e_tiles[c], rec_tiles[c], a_tiles[c], 0)
 
-            if 2 <= p < N_UNITS + 2:
-                g, w = divmod(p - 2, 2)
-                if (p - 2) % HEAD_UNITS == 0:
+            for y in range(2):
+                if p == attn_ready(y):
+                    quantise_attn(y)
+            if v_now:
+                quantise_values(o, qd, v_grp)
+            if 0 <= p < N_GROUPS:
+                w_quant[p] = quantise_w(w_grp[p])
+
+            g = p - MX_LAG
+            if 0 <= g < N_GROUPS:
+                if g % HEAD_GROUPS == 0:
                     vt_new = work.tile([P, 2, B, HEAD_GROUPS, I], BF16, name="vt")
                     vt[g // HEAD_GROUPS] = vt_new
-                project(g, w, w_quant[p - 2][0], w_quant[p - 2][1], vt[g // HEAD_GROUPS])
+                project(g, w_quant[g][0], w_quant[g][1], vt[g // HEAD_GROUPS])
             for o in range(O):
                 for y in range(2):
-                    if p == max(HEAD_UNITS * o + 22 + 4 * y, A_FIRST + 24 * y + 24):
+                    if p == finish_period(o, y):
                         finish(o, y)
-
-            if chunk_now:
-                if phase == 0:
-                    e_tiles[c] = attn_exp(c)
-                if phase == 1:
-                    rec_tiles[c] = attn_reciprocal(e_tiles[c])
-                if phase == 2:
-                    a_new = work.tile([P, 4, 2, 8, I], BF16, name="a_n")
-                    a_tiles[c] = a_new
-                    attn_scale(e_tiles[c], rec_tiles[c], a_tiles[c], 0)
-                if phase == 3:
-                    attn_scale(e_tiles[c], rec_tiles[c], a_tiles[c], 1)
-                if phase == 5 and c % 4 == 3:
-                    quantise_attn(c // 4)

@@ -26,7 +26,7 @@ MX_LAG = 2
 A_FIRST = 3
 A_CHUNKS = 8
 A_EVERY = 3
-V_FIRST = HEAD_GROUPS + MX_LAG
+V_FIRST = HEAD_GROUPS + MX_LAG + 1
 
 FLOPS = 2 * ROWS * O * FS * FS + 2 * B * O * LQ * I * LS * D
 
@@ -48,8 +48,7 @@ def tile_localcrossattention_pa_kernel(tc, scores, final_encoder_out, WV_w, WV_b
         w_bf = ctx.enter_context(tc.tile_pool(name="w_bf", bufs=2))
         w_mx = ctx.enter_context(tc.tile_pool(name="w_mx", bufs=MX_LAG + 2))
         work = ctx.enter_context(tc.tile_pool(name="work", bufs=2))
-        ps_t = ctx.enter_context(tc.psum_pool(name="ps_t", bufs=6))
-        ps_acc = ctx.enter_context(tc.psum_pool(name="ps_acc", bufs=2))
+        psum = ctx.enter_context(tc.psum_pool(name="psum", bufs=8))
 
         ctx.enter_context(tc.manual_schedule())
 
@@ -80,7 +79,7 @@ def tile_localcrossattention_pa_kernel(tc, scores, final_encoder_out, WV_w, WV_b
         o_sb = const.tile([P, O, 4, 4, D], F32)
 
         def transpose_two_passes(words, first_pass, grouped_words, on_scalar):
-            bank = ps_t.tile([P, 2, 2, P], F32, name="bank", tag="bank")
+            bank = psum.tile([P, 2, 2, P], F32, name="bank", tag="bank")
             for c in range(2):
                 for u in range(2):
                     blk = 2 * (first_pass + c) + u
@@ -124,7 +123,7 @@ def tile_localcrossattention_pa_kernel(tc, scores, final_encoder_out, WV_w, WV_b
             return w_codes, w_scales
 
         def project(g, w_codes, w_scales, vt):
-            acc = ps_acc.tile([P, 2, ROWS], F32, name="acc", tag="acc")
+            acc = psum.tile([P, 2, ROWS], F32, name="acc", tag="bank")
             for w in range(2):
                 for c in range(PASSES):
                     nc.tensor.matmul_mx(
@@ -146,7 +145,7 @@ def tile_localcrossattention_pa_kernel(tc, scores, final_encoder_out, WV_w, WV_b
                 )
 
         def values_quarter(o, qd, vt):
-            bank = ps_t.tile([P, 4, 2, P], BF16, name="v_bank", tag="bank")
+            bank = psum.tile([P, 4, 2, P], BF16, name="v_bank", tag="bank")
             for b4 in range(4):
                 for w in range(2):
                     nc.tensor.transpose(
@@ -191,7 +190,7 @@ def tile_localcrossattention_pa_kernel(tc, scores, final_encoder_out, WV_w, WV_b
 
         def attn_transpose(c, a_n):
             y, qp = divmod(c, 4)
-            bank = ps_t.tile([P, 8, P], BF16, name="a_bank", tag="bank")
+            bank = psum.tile([P, 8, P], BF16, name="a_bank", tag="bank")
             for l in range(2):
                 for t in range(4):
                     nc.tensor.transpose(
@@ -207,7 +206,7 @@ def tile_localcrossattention_pa_kernel(tc, scores, final_encoder_out, WV_w, WV_b
             )
 
         def finish(o, y):
-            res = ps_acc.tile([P, 2, 4, 2, 32], F32, name="res", tag="acc")
+            res = psum.tile([P, 2, 4, 2, 32], F32, name="res", tag="bank")
             for gl in range(2):
                 x0 = 8 * o + 4 * gl
                 b0 = 8 * y + 4 * gl
@@ -262,7 +261,7 @@ def tile_localcrossattention_pa_kernel(tc, scores, final_encoder_out, WV_w, WV_b
                         grp_words[:, 2 * half : 2 * half + 2, P * h : P * (h + 1), :],
                         on_scalar=(half == 0),
                     )
-            bias_bank = ps_t.tile([P, P], F32, name="bias_bank", tag="bank")
+            bias_bank = psum.tile([P, P], F32, name="bias_bank", tag="bank")
             nc.tensor.transpose(bias_bank[:], bias_raw[:].bitcast(F32), ident_f32[:])
             nc.vector.tensor_copy(
                 out=bias_sb[:],

@@ -23,7 +23,7 @@ N_GROUPS = O * FS // (2 * P)
 HEAD_GROUPS = N_GROUPS // O
 W_AHEAD = 4
 MX_LAG = 2
-A_FIRST = 3
+A_FIRST = 6
 A_CHUNKS = 8
 A_EVERY = 3
 V_FIRST = HEAD_GROUPS + MX_LAG + 1
@@ -235,19 +235,16 @@ def tile_localcrossattention_pa_kernel(tc, scores, final_encoder_out, WV_w, WV_b
         e_tiles = {}
         rec_tiles = {}
         a_tiles = {}
+        v_tiles = {}
         w_raw[0] = load_w(0)
         enc_raw = const.tile([P, 2, FS], BF16)
         nc.sync.dma_start(out=enc_raw[:], in_=enc_rows)
         bias_raw = const.tile([P, 2 * P], BF16)
         nc.vector.memset(bias_raw[:], 0.0)
         nc.sync.dma_start(out=bias_raw[0:N_GROUPS, :], in_=bias_rows)
-        w_raw[1] = load_w(1)
+        for g in range(1, W_AHEAD):
+            w_raw[g] = load_w(g)
         load_scores(0)
-        load_scores(1)
-        w_raw[2] = load_w(2)
-        load_scores(2)
-        load_scores(3)
-        w_raw[3] = load_w(3)
 
         def prepare_enc_and_bias():
             enc_grp = const.tile([P, PASSES, ROWS, 4], BF16, align_bytes=64)
@@ -286,8 +283,11 @@ def tile_localcrossattention_pa_kernel(tc, scores, final_encoder_out, WV_w, WV_b
         for p in range(finish_period(O - 1, 1) + 1):
             if 0 <= p < N_GROUPS - W_AHEAD:
                 w_raw[p + W_AHEAD] = load_w(p + W_AHEAD)
-            if 0 <= p < 4:
-                load_scores(p + 4)
+            if p + 1 < 8:
+                load_scores(p + 1)
+
+            if 1 <= p <= N_GROUPS:
+                w_quant[p - 1] = quantise_w(w_grp[p - 1])
 
             if 0 <= p < N_GROUPS:
                 w_grp[p] = transpose_w(w_raw[p])
@@ -299,7 +299,7 @@ def tile_localcrossattention_pa_kernel(tc, scores, final_encoder_out, WV_w, WV_b
             o, qd = divmod(p - V_FIRST, HEAD_GROUPS)
             v_now = 0 <= o < O and qd < 4
             if v_now:
-                v_grp = values_quarter(o, qd, vt[o])
+                v_tiles[o, qd] = values_quarter(o, qd, vt[o])
 
             c = chunk_at(p, 0)
             if c is not None:
@@ -319,10 +319,9 @@ def tile_localcrossattention_pa_kernel(tc, scores, final_encoder_out, WV_w, WV_b
             for y in range(2):
                 if p == attn_ready(y):
                     quantise_attn(y)
-            if v_now:
-                quantise_values(o, qd, v_grp)
-            if 0 <= p < N_GROUPS:
-                w_quant[p] = quantise_w(w_grp[p])
+            o, qd = divmod(p - 1 - V_FIRST, HEAD_GROUPS)
+            if 0 <= o < O and qd < 4:
+                quantise_values(o, qd, v_tiles[o, qd])
 
             g = p - MX_LAG
             if 0 <= g < N_GROUPS:

@@ -21,12 +21,14 @@ PASSES = FS // 512
 ROWS = B * I
 N_GROUPS = O * FS // (2 * P)
 HEAD_GROUPS = N_GROUPS // O
+HALF_GROUPS = HEAD_GROUPS // 2
+N_HALVES = 2 * O
 W_AHEAD = 4
 MX_LAG = 2
 A_FIRST = 6
 A_CHUNKS = 8
 A_EVERY = 3
-V_FIRST = HEAD_GROUPS + MX_LAG + 1
+V_LAG = HALF_GROUPS + MX_LAG
 
 FLOPS = 2 * ROWS * O * FS * FS + 2 * B * O * LQ * I * LS * D
 
@@ -34,12 +36,12 @@ FLOPS = 2 * ROWS * O * FS * FS + 2 * B * O * LQ * I * LS * D
 def tile_localcrossattention_pa_kernel(tc, scores, final_encoder_out, WV_w, WV_b, out):
     nc = tc.nc
 
-    w_groups = WV_w.rearrange("o (g j w) f -> (o g) j w f", j=P, w=2)
+    w_groups = WV_w.rearrange("o (g p h w) f -> o h g p w f", p=P, h=2, w=2)
     enc_rows = final_encoder_out.rearrange("b (i s) d -> (b i) (s d)", i=I).rearrange(
         "(h r) f -> r h f", h=2
     )
     score_rows = scores.rearrange("(y b) o i (h l) k -> y h (b o) i (l k)", y=2, h=4)
-    bias_rows = WV_b.rearrange("o (g x) -> (o g) x", x=2 * P)
+    bias_rows = WV_b.rearrange("o (g x) -> (o g) x", x=4 * P)
     out_rows = out.rearrange("(g b) (o q) d -> o b q g d", b=4, o=O)
 
     with ExitStack() as ctx:
@@ -54,36 +56,34 @@ def tile_localcrossattention_pa_kernel(tc, scores, final_encoder_out, WV_w, WV_b
 
         ident_f32 = const.tile([P, P], F32)
         make_identity(nc, ident_f32[:])
-        ident_bf = const.tile([P, P], BF16)
-        make_identity(nc, ident_bf[:])
-        perm_v = const.tile([P, P], BF16)
+        perm_w = const.tile([P, P], F32)
         nc.vector.tensor_copy(
-            out=perm_v[:].rearrange("p (c t) -> p c t", t=4),
-            in_=ident_bf[:].rearrange("p (t c) -> p c t", t=4),
+            out=perm_w[:].rearrange("p (q y u) -> p q y u", q=4, u=2),
+            in_=ident_f32[:].rearrange("p (q u y) -> p q y u", q=4, u=2),
         )
-        perm_a = const.tile([P, P], BF16)
+        perm_a = const.tile([P, P], F32)
         nc.vector.tensor_copy(
             out=perm_a[:].rearrange("p (o b h) -> p o b h", o=O, b=8),
-            in_=ident_bf[:].rearrange("p (b o h) -> p o b h", b=8, o=O),
+            in_=ident_f32[:].rearrange("p (b o h) -> p o b h", b=8, o=O),
         )
 
         enc_codes = const.tile([P, PASSES, ROWS], U32, align_bytes=64)
         enc_scales = const.tile([P, PASSES, ROWS], U8, align_bytes=64)
-        bias_sb = const.tile([P, N_GROUPS, 2], F32)
+        bias_sb = const.tile([P, O * HALF_GROUPS, 2, 2], F32)
         s_raw = const.tile([P, 2, I, 8 * LS], BF16)
-        a_grp = const.tile([P, 2, 32, 4, 4, 8], BF16, align_bytes=64)
+        a_grp = const.tile([P, 2, 32, 4, 4, 2, 2, 2], BF16, align_bytes=64)
         a_codes = const.tile([P, 2, 32, LQ], U32, align_bytes=64)
         a_scales = const.tile([P, 2, 32, LQ], U8, align_bytes=64)
-        v_codes = const.tile([P, O, B, D], U32, align_bytes=64)
-        v_scales = const.tile([P, O, B, D], U8, align_bytes=64)
+        v_codes = const.tile([P, O, 2, 4, 2 * 4 * 16], U32, align_bytes=64)
+        v_scales = const.tile([P, O, 2, 4, 2 * 4 * 16], U8, align_bytes=64)
         o_sb = const.tile([P, O, 4, 4, D], F32)
 
-        def transpose_two_passes(words, first_pass, grouped_words, on_scalar):
+        def transpose_two_passes(words, first_pass, grouped_words, perm, on_scalar):
             bank = psum.tile([P, 2, 2, P], F32, name="bank", tag="bank")
             for c in range(2):
                 for u in range(2):
                     blk = 2 * (first_pass + c) + u
-                    nc.tensor.transpose(bank[:, c, u, :], words[:, blk * P : (blk + 1) * P], ident_f32[:])
+                    nc.tensor.transpose(bank[:, c, u, :], words[:, blk * P : (blk + 1) * P], perm)
             if on_scalar:
                 nc.scalar.copy(out=grouped_words, in_=bank[:].rearrange("p c u n -> p c n u"))
             else:
@@ -91,7 +91,7 @@ def tile_localcrossattention_pa_kernel(tc, scores, final_encoder_out, WV_w, WV_b
 
         def load_w(g):
             w_raw = w_in.tile([P, 2, FS], BF16, name="w_raw")
-            nc.sync.dma_start(out=w_raw[:], in_=w_groups[g])
+            nc.sync.dma_start(out=w_raw[:], in_=w_groups[g // 8, g // 4 % 2, g % 4])
             return w_raw
 
         def load_scores(s):
@@ -108,6 +108,7 @@ def tile_localcrossattention_pa_kernel(tc, scores, final_encoder_out, WV_w, WV_b
                         raw_words[:, w, :],
                         2 * half,
                         grp_words[:, w, 2 * half : 2 * half + 2, :, :],
+                        perm_w[:],
                         on_scalar=(2 * w + half < 3),
                     )
             return w_grp
@@ -137,94 +138,103 @@ def tile_localcrossattention_pa_kernel(tc, scores, final_encoder_out, WV_w, WV_b
                     )
             for w in range(2):
                 nc.scalar.activation(
-                    out=vt[:, w, :, g % HEAD_GROUPS, :],
-                    in_=acc[:, w, :].rearrange("p (b i) -> p b i", i=I),
+                    out=vt[:, :, w, :, g % 4, :],
+                    in_=acc[:, w, :].rearrange("p (a b i) -> p a b i", a=4, i=I),
                     func=ACT.Identity,
-                    bias=bias_sb[:, g, w : w + 1],
+                    bias=bias_sb[:, 4 * (g // HEAD_GROUPS) + g % 4, g // 4 % 2, w : w + 1],
                     scale=1.0,
                 )
 
-        def values_quarter(o, qd, vt):
-            bank = psum.tile([P, 4, 2, P], BF16, name="v_bank", tag="bank")
-            for b4 in range(4):
-                for w in range(2):
-                    nc.tensor.transpose(
-                        bank[:, b4, w, :],
-                        vt[:, w, 4 * qd + b4].rearrange("p k i -> p (k i)"),
-                        perm_v[:],
-                    )
-            v_grp = work.tile([P, 4, 2, P], BF16, name="v_grp", align_bytes=64)
-            nc.vector.tensor_copy(out=v_grp[:], in_=bank[:])
-            return v_grp
+        def transpose_values(half, vt, v_grp):
+            nc.vector.transpose(
+                out=v_grp[:, 2 * half : 2 * half + 2].rearrange("p a x -> p (a x)").bitcast(F32),
+                in_=vt[:, 2 * half : 2 * half + 2].rearrange("p a w b g i -> p (a w b g i)").bitcast(F32),
+            )
 
-        def quantise_values(o, qd, v_grp):
+        def quantise_values(o, h, half, v_grp):
+            rng = slice(2 * half, 2 * half + 2)
             nc.vector.quantize_mx(
-                out=v_codes[:, o, 4 * qd : 4 * qd + 4, :].rearrange("p b n -> p (b n)").bitcast(FP8X4),
-                scales=v_scales[:, o, 4 * qd : 4 * qd + 4, :].rearrange("p b n -> p (b n)"),
-                in_=v_grp[:].rearrange("p b w n -> p (b w n)"),
+                out=v_codes[:, o, h, rng, :].rearrange("p a n -> p (a n)").bitcast(FP8X4),
+                scales=v_scales[:, o, h, rng, :].rearrange("p a n -> p (a n)"),
+                in_=v_grp[:, rng].rearrange("p a x -> p (a x)"),
             )
 
         def attn_exp(c):
             y, qp = divmod(c, 4)
-            e_t = work.tile([P, I, 2 * LS], F32, name="e_t")
-            nc.scalar.activation(out=e_t[:], in_=s_raw[:, y, :, 64 * qp : 64 * qp + 64], func=ACT.Exp)
+            e_t = work.tile([P, 2 * 4, I, 8], F32, name="e_t")
+            nc.scalar.activation(
+                out=e_t[:],
+                in_=s_raw[:, y, :, 64 * qp : 64 * qp + 64].rearrange("p i (m k) -> p m i k", k=8),
+                func=ACT.Exp,
+            )
             return e_t
 
         def attn_reciprocal(e_t):
-            ssum = work.tile([P, I, 2], F32, name="ssum")
+            ssum = work.tile([P, 2, I], F32, name="ssum")
             nc.vector.tensor_reduce(
-                out=ssum[:], in_=e_t[:].rearrange("p i (l k) -> p i l k", k=LS), axis=AXIS.X, op=ALU.add
+                out=ssum[:], in_=e_t[:].rearrange("p (l g) i k -> p l i g k", l=2), axis=AXIS.XY, op=ALU.add
             )
             nc.vector.tensor_scalar_add(out=ssum[:], in0=ssum[:], scalar1=EPS)
-            rec = work.tile([P, I, 2], F32, name="rec")
-            nc.vector.reciprocal(out=rec[:], in_=ssum[:])
+            rec = work.tile([P, 2, 4 * I], F32, name="rec")
+            nc.vector.reciprocal(
+                out=rec[:].rearrange("p l (g i) -> p l g i", g=4),
+                in_=ssum[:].unsqueeze(2).to_broadcast([P, 2, 4, I]),
+            )
             return rec
 
         def attn_scale(e_t, rec, a_n, l):
             nc.vector.tensor_tensor(
-                out=a_n[:, :, l].rearrange("p t k i -> p k i t"),
-                in0=e_t[:, :, LS * l : LS * (l + 1)].rearrange("p i (k t) -> p k i t", t=4),
-                in1=rec[:, :, l].unsqueeze(1).unsqueeze(3).to_broadcast([P, 8, I, 4]),
+                out=a_n[:, l].rearrange("p u q g i -> p q (g i) u"),
+                in0=e_t[:, 4 * l : 4 * l + 4].rearrange("p g i (q u) -> p q (g i) u", u=2),
+                in1=rec[:, l, :].unsqueeze(1).unsqueeze(3).to_broadcast([P, 4, 4 * I, 2]),
                 op=ALU.mult,
             )
 
         def attn_transpose(c, a_n):
             y, qp = divmod(c, 4)
-            bank = psum.tile([P, 8, P], BF16, name="a_bank", tag="bank")
+            bank = psum.tile([P, 4, P], F32, name="a_bank", tag="bank")
             for l in range(2):
-                for t in range(4):
+                for u in range(2):
                     nc.tensor.transpose(
-                        bank[:, 4 * l + t, :], a_n[:, t, l].rearrange("p k i -> p (k i)"), perm_a[:]
+                        bank[:, 2 * l + u, :],
+                        a_n[:, l, u].rearrange("p q g i -> p (q g i)").bitcast(F32),
+                        perm_a[:],
                     )
-            nc.scalar.copy(out=a_grp[:, y, :, :, qp, :], in_=bank[:].rearrange("p s (x h) -> p x h s", h=4))
+            nc.scalar.copy(
+                out=a_grp[:, y].rearrange("p x h r l u e -> p x h r (l u e)").bitcast(F32)[:, :, :, qp, :],
+                in_=bank[:].rearrange("p s (x h) -> p x h s", h=4),
+            )
 
         def quantise_attn(y):
             nc.vector.quantize_mx(
                 out=a_codes[:, y].rearrange("p x q -> p (x q)").bitcast(FP8X4),
                 scales=a_scales[:, y].rearrange("p x q -> p (x q)"),
-                in_=a_grp[:, y].rearrange("p x h g s -> p (x h g s)"),
+                in_=a_grp[:, y].rearrange("p x h r l u e -> p (x h r l u e)"),
             )
 
         def finish(o, y):
-            res = psum.tile([P, 2, 4, 2, 32], F32, name="res", tag="bank")
+            res = psum.tile([P, 2, 4, 4, 16], F32, name="res", tag="bank")
             for gl in range(2):
+                a = 2 * y + gl
                 x0 = 8 * o + 4 * gl
-                b0 = 8 * y + 4 * gl
-                nc.tensor.matmul_mx(
-                    out=res[:, gl].rearrange("p b w c -> p (b w c)"),
-                    lhsT=a_codes[:, y, x0 : x0 + 4, :].rearrange("p x q -> p (x q)").bitcast(FP8X4),
-                    lhsT_scale=a_scales[:, y, x0 : x0 + 4, :].rearrange("p x q -> p (x q)"),
-                    rhs=v_codes[:, o, b0 : b0 + 4, :].rearrange("p b n -> p (b n)").bitcast(FP8X4),
-                    rhs_scale=v_scales[:, o, b0 : b0 + 4, :].rearrange("p b n -> p (b n)"),
-                    start=True,
-                    stop=True,
-                )
-            dst = o_sb[:, o, 2 * y : 2 * y + 2].rearrange("p g b (c w) -> p (g b) c w", w=2)
-            src = res[:].rearrange("p g b w c -> p (g b) c w")
-            if y == 0:
-                nc.scalar.mul(out=dst, in_=src, mul=COEFF)
-            else:
-                nc.vector.tensor_scalar(out=dst, in0=src, scalar1=COEFF, scalar2=None, op0=ALU.mult)
+                for h in range(2):
+                    nc.tensor.matmul_mx(
+                        out=res[:, gl, 2 * h : 2 * h + 2].rearrange("p w b y -> p (w b y)"),
+                        lhsT=a_codes[:, y, x0 : x0 + 4, :].rearrange("p x q -> p (x q)").bitcast(FP8X4),
+                        lhsT_scale=a_scales[:, y, x0 : x0 + 4, :].rearrange("p x q -> p (x q)"),
+                        rhs=v_codes[:, o, h, a, :].bitcast(FP8X4),
+                        rhs_scale=v_scales[:, o, h, a, :],
+                        start=True,
+                        stop=True,
+                    )
+            for gl in range(2):
+                dst = o_sb[:, o, 2 * y + gl].rearrange("p b (y m) -> p b y m", m=4)
+                src = res[:, gl].rearrange("p m b y -> p b y m")
+                if y == 0:
+                    nc.scalar.mul(out=dst, in_=src, mul=COEFF)
+                else:
+                    nc.vector.tensor_scalar(out=dst, in0=src, scalar1=COEFF, scalar2=None, op0=ALU.mult)
+            if y == 1:
                 for b4 in range(4):
                     nc.sync.dma_start(out=out_rows[o, b4], in_=o_sb[32 * b4 : 32 * b4 + 32, o, :, b4, :])
 
@@ -239,9 +249,9 @@ def tile_localcrossattention_pa_kernel(tc, scores, final_encoder_out, WV_w, WV_b
         w_raw[0] = load_w(0)
         enc_raw = const.tile([P, 2, FS], BF16)
         nc.sync.dma_start(out=enc_raw[:], in_=enc_rows)
-        bias_raw = const.tile([P, 2 * P], BF16)
+        bias_raw = const.tile([P, 4 * P], BF16)
         nc.vector.memset(bias_raw[:], 0.0)
-        nc.sync.dma_start(out=bias_raw[0:N_GROUPS, :], in_=bias_rows)
+        nc.sync.dma_start(out=bias_raw[0 : O * HALF_GROUPS, :], in_=bias_rows)
         for g in range(1, W_AHEAD):
             w_raw[g] = load_w(g)
         load_scores(0)
@@ -256,13 +266,20 @@ def tile_localcrossattention_pa_kernel(tc, scores, final_encoder_out, WV_w, WV_b
                         raw_words[:, h, :],
                         2 * half,
                         grp_words[:, 2 * half : 2 * half + 2, P * h : P * (h + 1), :],
+                        ident_f32[:],
                         on_scalar=(half == 0),
                     )
-            bias_bank = psum.tile([P, P], F32, name="bias_bank", tag="bank")
-            nc.tensor.transpose(bias_bank[:], bias_raw[:].bitcast(F32), ident_f32[:])
+            bias_ord = const.tile([P, 2, P], F32)
+            nc.vector.tensor_copy(
+                out=bias_ord[:].rearrange("p h (q y u) -> p h q y u", q=4, u=2),
+                in_=bias_raw[:].bitcast(F32).rearrange("p (q u y h) -> p h q y u", q=4, u=2, h=2),
+            )
+            bias_bank = psum.tile([P, 2, P], F32, name="bias_bank", tag="bank")
+            for h in range(2):
+                nc.tensor.transpose(bias_bank[:, h, :], bias_ord[:, h, :], ident_f32[:])
             nc.vector.tensor_copy(
                 out=bias_sb[:],
-                in_=bias_bank[:].bitcast(BF16).rearrange("p (g w) -> p g w", w=2)[:, 0:N_GROUPS, :],
+                in_=bias_bank[:].bitcast(BF16).rearrange("p h (r w) -> p r h w", w=2)[:, 0 : O * HALF_GROUPS],
             )
             nc.vector.quantize_mx(
                 out=enc_codes[:].rearrange("p c r -> p (c r)").bitcast(FP8X4),
@@ -278,7 +295,7 @@ def tile_localcrossattention_pa_kernel(tc, scores, final_encoder_out, WV_w, WV_b
             return A_FIRST + A_EVERY * (4 * y + 3) + 6
 
         def finish_period(o, y):
-            return max(HEAD_GROUPS * o + V_FIRST + 4 + y, attn_ready(y) + 1 + o)
+            return max(HALF_GROUPS * (2 * o + 1) + V_LAG + 3 + y, attn_ready(y) + 1 + o)
 
         for p in range(finish_period(O - 1, 1) + 1):
             if 0 <= p < N_GROUPS - W_AHEAD:
@@ -296,10 +313,12 @@ def tile_localcrossattention_pa_kernel(tc, scores, final_encoder_out, WV_w, WV_b
             c = chunk_at(p, 5)
             if c is not None:
                 attn_transpose(c, a_tiles[c])
-            o, qd = divmod(p - V_FIRST, HEAD_GROUPS)
-            v_now = 0 <= o < O and qd < 4
-            if v_now:
-                v_tiles[o, qd] = values_quarter(o, qd, vt[o])
+            hh, piece = divmod(p - V_LAG, HALF_GROUPS)
+            if 0 <= hh < N_HALVES and piece < 2:
+                if piece == 0:
+                    v_new = work.tile([P, 4, 4 * 2 * 4 * 16], BF16, name="v_grp", align_bytes=64)
+                    v_tiles[hh] = v_new
+                transpose_values(piece, vt[hh], v_tiles[hh])
 
             c = chunk_at(p, 0)
             if c is not None:
@@ -312,23 +331,23 @@ def tile_localcrossattention_pa_kernel(tc, scores, final_encoder_out, WV_w, WV_b
                 rec_tiles[c] = attn_reciprocal(e_tiles[c])
             c = chunk_at(p, 2)
             if c is not None:
-                a_new = work.tile([P, 4, 2, 8, I], BF16, name="a_n")
+                a_new = work.tile([P, 2, 2, 4, 4, I], BF16, name="a_n")
                 a_tiles[c] = a_new
                 attn_scale(e_tiles[c], rec_tiles[c], a_tiles[c], 0)
 
             for y in range(2):
                 if p == attn_ready(y):
                     quantise_attn(y)
-            o, qd = divmod(p - 1 - V_FIRST, HEAD_GROUPS)
-            if 0 <= o < O and qd < 4:
-                quantise_values(o, qd, v_tiles[o, qd])
+            hh, piece = divmod(p - 1 - V_LAG, HALF_GROUPS)
+            if 0 <= hh < N_HALVES and piece < 2:
+                quantise_values(hh // 2, hh % 2, piece, v_tiles[hh])
 
             g = p - MX_LAG
             if 0 <= g < N_GROUPS:
-                if g % HEAD_GROUPS == 0:
-                    vt_new = work.tile([P, 2, B, HEAD_GROUPS, I], BF16, name="vt")
-                    vt[g // HEAD_GROUPS] = vt_new
-                project(g, w_quant[g][0], w_quant[g][1], vt[g // HEAD_GROUPS])
+                if g % HALF_GROUPS == 0:
+                    vt_new = work.tile([P, 4, 2, 4, 4, I], BF16, name="vt", align_bytes=64)
+                    vt[g // HALF_GROUPS] = vt_new
+                project(g, w_quant[g][0], w_quant[g][1], vt[g // HALF_GROUPS])
             for o in range(O):
                 for y in range(2):
                     if p == finish_period(o, y):

@@ -50,6 +50,7 @@ def tile_localcrossattention_pa_kernel(tc, scores, final_encoder_out, WV_w, WV_b
         w_bf = ctx.enter_context(tc.tile_pool(name="w_bf", bufs=2))
         w_mx = ctx.enter_context(tc.tile_pool(name="w_mx", bufs=MX_LAG + 2))
         work = ctx.enter_context(tc.tile_pool(name="work", bufs=2))
+        attn = ctx.enter_context(tc.tile_pool(name="attn", bufs=3))
         psum = ctx.enter_context(tc.psum_pool(name="psum", bufs=8))
 
         ctx.enter_context(tc.manual_schedule())
@@ -98,7 +99,7 @@ def tile_localcrossattention_pa_kernel(tc, scores, final_encoder_out, WV_w, WV_b
             y, h = divmod(s, 4)
             nc.sync.dma_start(out=s_raw[h:P:4, y], in_=score_rows[y, h])
 
-        def transpose_w(w_raw):
+        def transpose_w(p, w_raw):
             w_grp = w_bf.tile([P, 2, PASSES, P, 4], BF16, name="w_grp", align_bytes=64)
             raw_words = w_raw[:].bitcast(F32)
             grp_words = w_grp[:].bitcast(F32)
@@ -109,7 +110,7 @@ def tile_localcrossattention_pa_kernel(tc, scores, final_encoder_out, WV_w, WV_b
                         2 * half,
                         grp_words[:, w, 2 * half : 2 * half + 2, :, :],
                         perm_w[:],
-                        on_scalar=(2 * w + half < 3),
+                        on_scalar=not (w == 0 and half == 1 and chunk_at(p, 1) is None),
                     )
             return w_grp
 
@@ -161,7 +162,7 @@ def tile_localcrossattention_pa_kernel(tc, scores, final_encoder_out, WV_w, WV_b
 
         def attn_exp(c):
             y, qp = divmod(c, 4)
-            e_t = work.tile([P, 2 * 4, I, 8], F32, name="e_t")
+            e_t = attn.tile([P, 2 * 4, I, 8], F32, name="e_t")
             nc.scalar.activation(
                 out=e_t[:],
                 in_=s_raw[:, y, :, 64 * qp : 64 * qp + 64].rearrange("p i (m k) -> p m i k", k=8),
@@ -169,16 +170,28 @@ def tile_localcrossattention_pa_kernel(tc, scores, final_encoder_out, WV_w, WV_b
             )
             return e_t
 
-        def attn_reciprocal(e_t):
-            ssum = work.tile([P, 2, I], F32, name="ssum")
+        def attn_sum(e_t):
+            ssum = attn.tile([P, 2, I], F32, name="ssum")
             nc.vector.tensor_reduce(
                 out=ssum[:], in_=e_t[:].rearrange("p (l g) i k -> p l i g k", l=2), axis=AXIS.XY, op=ALU.add
             )
-            nc.vector.tensor_scalar_add(out=ssum[:], in0=ssum[:], scalar1=EPS)
-            rec = work.tile([P, 2, 4 * I], F32, name="rec")
-            nc.vector.reciprocal(
+            denom = attn.tile([P, 2, I], F32, name="denom")
+            nc.gpsimd.tensor_scalar(
+                out=denom[:], in0=ssum[:], scalar1=EPS, scalar2=1.0, op0=ALU.add, op1=ALU.mult
+            )
+            return denom
+
+        def attn_reciprocal(denom):
+            small = attn.tile([P, 2, I], F32, name="small")
+            nc.vector.reciprocal(out=small[:], in_=denom[:])
+            rec = attn.tile([P, 2, 4 * I], F32, name="rec")
+            nc.gpsimd.tensor_scalar(
                 out=rec[:].rearrange("p l (g i) -> p l g i", g=4),
-                in_=ssum[:].unsqueeze(2).to_broadcast([P, 2, 4, I]),
+                in0=small[:].unsqueeze(2).to_broadcast([P, 2, 4, I]),
+                scalar1=1.0,
+                scalar2=0.0,
+                op0=ALU.mult,
+                op1=ALU.add,
             )
             return rec
 
@@ -243,6 +256,7 @@ def tile_localcrossattention_pa_kernel(tc, scores, final_encoder_out, WV_w, WV_b
         w_quant = {}
         vt = {}
         e_tiles = {}
+        den_tiles = {}
         rec_tiles = {}
         a_tiles = {}
         v_tiles = {}
@@ -306,8 +320,12 @@ def tile_localcrossattention_pa_kernel(tc, scores, final_encoder_out, WV_w, WV_b
             if 1 <= p <= N_GROUPS:
                 w_quant[p - 1] = quantise_w(w_grp[p - 1])
 
+            c = chunk_at(p, 2)
+            if c is not None:
+                rec_tiles[c] = attn_reciprocal(den_tiles[c])
+
             if 0 <= p < N_GROUPS:
-                w_grp[p] = transpose_w(w_raw[p])
+                w_grp[p] = transpose_w(p, w_raw[p])
             if p == 0:
                 prepare_enc_and_bias()
             c = chunk_at(p, 5)
@@ -325,15 +343,15 @@ def tile_localcrossattention_pa_kernel(tc, scores, final_encoder_out, WV_w, WV_b
                 e_tiles[c] = attn_exp(c)
             c = chunk_at(p, 3)
             if c is not None:
+                a_new = attn.tile([P, 2, 2, 4, 4, I], BF16, name="a_n")
+                a_tiles[c] = a_new
+                attn_scale(e_tiles[c], rec_tiles[c], a_tiles[c], 0)
+            c = chunk_at(p, 4)
+            if c is not None:
                 attn_scale(e_tiles[c], rec_tiles[c], a_tiles[c], 1)
             c = chunk_at(p, 1)
             if c is not None:
-                rec_tiles[c] = attn_reciprocal(e_tiles[c])
-            c = chunk_at(p, 2)
-            if c is not None:
-                a_new = work.tile([P, 2, 2, 4, 4, I], BF16, name="a_n")
-                a_tiles[c] = a_new
-                attn_scale(e_tiles[c], rec_tiles[c], a_tiles[c], 0)
+                den_tiles[c] = attn_sum(e_tiles[c])
 
             for y in range(2):
                 if p == attn_ready(y):

@@ -25,9 +25,7 @@ HALF_GROUPS = HEAD_GROUPS // 2
 N_HALVES = 2 * O
 W_AHEAD = 4
 MX_LAG = 2
-A_FIRST = 6
-A_CHUNKS = 8
-A_EVERY = 3
+A_STARTS = [0, 1, 3, 6, 10, 14, 18, 22]
 V_LAG = HALF_GROUPS + MX_LAG
 
 FLOPS = 2 * ROWS * O * FS * FS + 2 * B * O * LQ * I * LS * D
@@ -110,18 +108,19 @@ def tile_localcrossattention_pa_kernel(tc, scores, final_encoder_out, WV_w, WV_b
                         2 * half,
                         grp_words[:, w, 2 * half : 2 * half + 2, :, :],
                         perm_w[:],
-                        on_scalar=not (w == 0 and half == 1 and chunk_at(p, 1) is None),
+                        on_scalar=not (w == 0 and half == 1 and chunk_at(p, 4) is None),
                     )
             return w_grp
 
-        def quantise_w(w_grp):
+        def quantise_w(w_grp, last):
             w_codes = w_mx.tile([P, 2, PASSES, P], U32, name="w_codes", align_bytes=64)
             w_scales = w_mx.tile([P, 2, PASSES, P], U8, name="w_scales", align_bytes=64)
-            nc.vector.quantize_mx(
-                out=w_codes[:].rearrange("p w c n -> p (w c n)").bitcast(FP8X4),
-                scales=w_scales[:].rearrange("p w c n -> p (w c n)"),
-                in_=w_grp[:].rearrange("p w c n t -> p (w c n t)"),
-            )
+            for part in (slice(0, 1), slice(1, 2)) if last else (slice(0, 2),):
+                nc.vector.quantize_mx(
+                    out=w_codes[:, part].rearrange("p w c n -> p (w c n)").bitcast(FP8X4),
+                    scales=w_scales[:, part].rearrange("p w c n -> p (w c n)"),
+                    in_=w_grp[:, part].rearrange("p w c n t -> p (w c n t)"),
+                )
             return w_codes, w_scales
 
         def project(g, w_codes, w_scales, vt):
@@ -225,7 +224,7 @@ def tile_localcrossattention_pa_kernel(tc, scores, final_encoder_out, WV_w, WV_b
                 in_=a_grp[:, y].rearrange("p x h r l u e -> p (x h r l u e)"),
             )
 
-        def finish(o, y):
+        def finish_passes(o, y):
             res = psum.tile([P, 2, 4, 4, 16], F32, name="res", tag="bank")
             for gl in range(2):
                 a = 2 * y + gl
@@ -240,10 +239,13 @@ def tile_localcrossattention_pa_kernel(tc, scores, final_encoder_out, WV_w, WV_b
                         start=True,
                         stop=True,
                     )
+            return res
+
+        def finish_copies(o, y, res):
             for gl in range(2):
                 dst = o_sb[:, o, 2 * y + gl].rearrange("p b (y m) -> p b y m", m=4)
                 src = res[:, gl].rearrange("p m b y -> p b y m")
-                if y == 0:
+                if gl == 0:
                     nc.scalar.mul(out=dst, in_=src, mul=COEFF)
                 else:
                     nc.vector.tensor_scalar(out=dst, in0=src, scalar1=COEFF, scalar2=None, op0=ALU.mult)
@@ -260,15 +262,21 @@ def tile_localcrossattention_pa_kernel(tc, scores, final_encoder_out, WV_w, WV_b
         rec_tiles = {}
         a_tiles = {}
         v_tiles = {}
-        w_raw[0] = load_w(0)
+        results = {}
+        w_new = w_in.tile([P, 2, FS], BF16, name="w_raw")
+        for w in range(2):
+            nc.sync.dma_start(out=w_new[:, w, :], in_=w_groups[0, 0, 0][:, w, :])
+        w_raw[0] = w_new
         enc_raw = const.tile([P, 2, FS], BF16)
         nc.sync.dma_start(out=enc_raw[:], in_=enc_rows)
         bias_raw = const.tile([P, 4 * P], BF16)
         nc.vector.memset(bias_raw[:], 0.0)
         nc.sync.dma_start(out=bias_raw[0 : O * HALF_GROUPS, :], in_=bias_rows)
-        for g in range(1, W_AHEAD):
-            w_raw[g] = load_w(g)
-        load_scores(0)
+        for s in range(4):
+            load_scores(s)
+        w_raw[1] = load_w(1)
+        w_raw[2] = load_w(2)
+        w_raw[3] = load_w(3)
 
         def prepare_enc_and_bias():
             enc_grp = const.tile([P, PASSES, ROWS, 4], BF16, align_bytes=64)
@@ -302,11 +310,11 @@ def tile_localcrossattention_pa_kernel(tc, scores, final_encoder_out, WV_w, WV_b
             )
 
         def chunk_at(p, offset):
-            c, rest = divmod(p - A_FIRST - offset, A_EVERY)
-            return c if rest == 0 and 0 <= c < A_CHUNKS else None
+            start = p - offset
+            return A_STARTS.index(start) if start in A_STARTS else None
 
         def attn_ready(y):
-            return A_FIRST + A_EVERY * (4 * y + 3) + 6
+            return A_STARTS[4 * y + 3] + 6
 
         def finish_period(o, y):
             return max(HALF_GROUPS * (2 * o + 1) + V_LAG + 3 + y, attn_ready(y) + 1 + o)
@@ -314,11 +322,11 @@ def tile_localcrossattention_pa_kernel(tc, scores, final_encoder_out, WV_w, WV_b
         for p in range(finish_period(O - 1, 1) + 1):
             if 0 <= p < N_GROUPS - W_AHEAD:
                 w_raw[p + W_AHEAD] = load_w(p + W_AHEAD)
-            if p + 1 < 8:
-                load_scores(p + 1)
+            if 4 <= p < 4 + 4:
+                load_scores(p - 4 + 4)
 
             if 1 <= p <= N_GROUPS:
-                w_quant[p - 1] = quantise_w(w_grp[p - 1])
+                w_quant[p - 1] = quantise_w(w_grp[p - 1], p == N_GROUPS)
 
             c = chunk_at(p, 2)
             if c is not None:
@@ -326,6 +334,9 @@ def tile_localcrossattention_pa_kernel(tc, scores, final_encoder_out, WV_w, WV_b
 
             if 0 <= p < N_GROUPS:
                 w_grp[p] = transpose_w(p, w_raw[p])
+            c = chunk_at(p, 0)
+            if c is not None:
+                e_tiles[c] = attn_exp(c)
             if p == 0:
                 prepare_enc_and_bias()
             c = chunk_at(p, 5)
@@ -338,9 +349,6 @@ def tile_localcrossattention_pa_kernel(tc, scores, final_encoder_out, WV_w, WV_b
                     v_tiles[hh] = v_new
                 transpose_values(piece, vt[hh], v_tiles[hh])
 
-            c = chunk_at(p, 0)
-            if c is not None:
-                e_tiles[c] = attn_exp(c)
             c = chunk_at(p, 3)
             if c is not None:
                 a_new = attn.tile([P, 2, 2, 4, 4, I], BF16, name="a_n")
@@ -369,4 +377,5 @@ def tile_localcrossattention_pa_kernel(tc, scores, final_encoder_out, WV_w, WV_b
             for o in range(O):
                 for y in range(2):
                     if p == finish_period(o, y):
-                        finish(o, y)
+                        results[o, y] = finish_passes(o, y)
+                        finish_copies(o, y, results[o, y])

@@ -174,23 +174,23 @@ def tile_localcrossattention_pa_kernel(tc, scores, final_encoder_out, WV_w, WV_b
             nc.vector.tensor_reduce(
                 out=ssum[:], in_=e_t[:].rearrange("p (l g) i k -> p l i g k", l=2), axis=AXIS.XY, op=ALU.add
             )
+            return ssum
+
+        def attn_eps(ssum):
             denom = attn.tile([P, 2, I], F32, name="denom")
-            nc.gpsimd.tensor_scalar(
-                out=denom[:], in0=ssum[:], scalar1=EPS, scalar2=1.0, op0=ALU.add, op1=ALU.mult
-            )
+            nc.vector.tensor_scalar_add(out=denom[:], in0=ssum[:], scalar1=EPS)
             return denom
 
         def attn_reciprocal(denom):
             small = attn.tile([P, 2, I], F32, name="small")
             nc.vector.reciprocal(out=small[:], in_=denom[:])
+            return small
+
+        def attn_repeat(small):
             rec = attn.tile([P, 2, 4 * I], F32, name="rec")
-            nc.gpsimd.tensor_scalar(
+            nc.vector.tensor_copy(
                 out=rec[:].rearrange("p l (g i) -> p l g i", g=4),
-                in0=small[:].unsqueeze(2).to_broadcast([P, 2, 4, I]),
-                scalar1=1.0,
-                scalar2=0.0,
-                op0=ALU.mult,
-                op1=ALU.add,
+                in_=small[:].unsqueeze(2).to_broadcast([P, 2, 4, I]),
             )
             return rec
 
@@ -258,7 +258,9 @@ def tile_localcrossattention_pa_kernel(tc, scores, final_encoder_out, WV_w, WV_b
         w_quant = {}
         vt = {}
         e_tiles = {}
+        sum_tiles = {}
         den_tiles = {}
+        small_tiles = {}
         rec_tiles = {}
         a_tiles = {}
         v_tiles = {}
@@ -330,7 +332,10 @@ def tile_localcrossattention_pa_kernel(tc, scores, final_encoder_out, WV_w, WV_b
 
             c = chunk_at(p, 2)
             if c is not None:
-                rec_tiles[c] = attn_reciprocal(den_tiles[c])
+                den_tiles[c] = attn_eps(sum_tiles[c])
+            c = chunk_at(p, 3)
+            if c is not None:
+                rec_tiles[c] = attn_repeat(small_tiles[c])
 
             if 0 <= p < N_GROUPS:
                 w_grp[p] = transpose_w(p, w_raw[p])
@@ -342,6 +347,9 @@ def tile_localcrossattention_pa_kernel(tc, scores, final_encoder_out, WV_w, WV_b
             c = chunk_at(p, 5)
             if c is not None:
                 attn_transpose(c, a_tiles[c])
+            c = chunk_at(p, 2)
+            if c is not None:
+                small_tiles[c] = attn_reciprocal(den_tiles[c])
             hh, piece = divmod(p - V_LAG, HALF_GROUPS)
             if 0 <= hh < N_HALVES and piece < 2:
                 if piece == 0:
@@ -359,7 +367,7 @@ def tile_localcrossattention_pa_kernel(tc, scores, final_encoder_out, WV_w, WV_b
                 attn_scale(e_tiles[c], rec_tiles[c], a_tiles[c], 1)
             c = chunk_at(p, 1)
             if c is not None:
-                den_tiles[c] = attn_sum(e_tiles[c])
+                sum_tiles[c] = attn_sum(e_tiles[c])
 
             for y in range(2):
                 if p == attn_ready(y):

@@ -25,8 +25,8 @@ HALF_GROUPS = HEAD_GROUPS // 2
 N_HALVES = 2 * O
 W_AHEAD = 4
 MX_LAG = 2
-A_STARTS = [0, 1, 3, 6, 10, 14, 18, 22]
-V_LAG = HALF_GROUPS + MX_LAG
+A_STARTS = [0, 0, 1, 4] + [HALF_GROUPS * n for n in (3, 4, 5, 6)]
+V_LAG = HALF_GROUPS + MX_LAG + 1
 
 FLOPS = 2 * ROWS * O * FS * FS + 2 * B * O * LQ * I * LS * D
 
@@ -48,7 +48,7 @@ def tile_localcrossattention_pa_kernel(tc, scores, final_encoder_out, WV_w, WV_b
         w_bf = ctx.enter_context(tc.tile_pool(name="w_bf", bufs=2))
         w_mx = ctx.enter_context(tc.tile_pool(name="w_mx", bufs=MX_LAG + 2))
         work = ctx.enter_context(tc.tile_pool(name="work", bufs=2))
-        attn = ctx.enter_context(tc.tile_pool(name="attn", bufs=3))
+        attn = ctx.enter_context(tc.tile_pool(name="attn", bufs=4))
         psum = ctx.enter_context(tc.psum_pool(name="psum", bufs=8))
 
         ctx.enter_context(tc.manual_schedule())
@@ -108,7 +108,7 @@ def tile_localcrossattention_pa_kernel(tc, scores, final_encoder_out, WV_w, WV_b
                         2 * half,
                         grp_words[:, w, 2 * half : 2 * half + 2, :, :],
                         perm_w[:],
-                        on_scalar=not (w == 0 and half == 1 and chunk_at(p, 4) is None),
+                        on_scalar=not (w == 1 and half == 1 and p < N_GROUPS - 2 and not chunks_at(p, 0)),
                     )
             return w_grp
 
@@ -311,9 +311,8 @@ def tile_localcrossattention_pa_kernel(tc, scores, final_encoder_out, WV_w, WV_b
                 in_=enc_grp[:].rearrange("p c r t -> p (c r t)"),
             )
 
-        def chunk_at(p, offset):
-            start = p - offset
-            return A_STARTS.index(start) if start in A_STARTS else None
+        def chunks_at(p, offset):
+            return [c for c, start in enumerate(A_STARTS) if start == p - offset]
 
         def attn_ready(y):
             return A_STARTS[4 * y + 3] + 6
@@ -330,25 +329,16 @@ def tile_localcrossattention_pa_kernel(tc, scores, final_encoder_out, WV_w, WV_b
             if 1 <= p <= N_GROUPS:
                 w_quant[p - 1] = quantise_w(w_grp[p - 1], p == N_GROUPS)
 
-            c = chunk_at(p, 2)
-            if c is not None:
+            for c in chunks_at(p, 2):
                 den_tiles[c] = attn_eps(sum_tiles[c])
-            c = chunk_at(p, 3)
-            if c is not None:
+            for c in chunks_at(p, 3):
                 rec_tiles[c] = attn_repeat(small_tiles[c])
 
             if 0 <= p < N_GROUPS:
                 w_grp[p] = transpose_w(p, w_raw[p])
-            c = chunk_at(p, 0)
-            if c is not None:
-                e_tiles[c] = attn_exp(c)
             if p == 0:
                 prepare_enc_and_bias()
-            c = chunk_at(p, 5)
-            if c is not None:
-                attn_transpose(c, a_tiles[c])
-            c = chunk_at(p, 2)
-            if c is not None:
+            for c in chunks_at(p, 2):
                 small_tiles[c] = attn_reciprocal(den_tiles[c])
             hh, piece = divmod(p - V_LAG, HALF_GROUPS)
             if 0 <= hh < N_HALVES and piece < 2:
@@ -357,21 +347,6 @@ def tile_localcrossattention_pa_kernel(tc, scores, final_encoder_out, WV_w, WV_b
                     v_tiles[hh] = v_new
                 transpose_values(piece, vt[hh], v_tiles[hh])
 
-            c = chunk_at(p, 3)
-            if c is not None:
-                a_new = attn.tile([P, 2, 2, 4, 4, I], BF16, name="a_n")
-                a_tiles[c] = a_new
-                attn_scale(e_tiles[c], rec_tiles[c], a_tiles[c], 0)
-            c = chunk_at(p, 4)
-            if c is not None:
-                attn_scale(e_tiles[c], rec_tiles[c], a_tiles[c], 1)
-            c = chunk_at(p, 1)
-            if c is not None:
-                sum_tiles[c] = attn_sum(e_tiles[c])
-
-            for y in range(2):
-                if p == attn_ready(y):
-                    quantise_attn(y)
             hh, piece = divmod(p - 1 - V_LAG, HALF_GROUPS)
             if 0 <= hh < N_HALVES and piece < 2:
                 quantise_values(hh // 2, hh % 2, piece, v_tiles[hh])
@@ -382,6 +357,23 @@ def tile_localcrossattention_pa_kernel(tc, scores, final_encoder_out, WV_w, WV_b
                     vt_new = work.tile([P, 4, 2, 4, 4, I], BF16, name="vt", align_bytes=64)
                     vt[g // HALF_GROUPS] = vt_new
                 project(g, w_quant[g][0], w_quant[g][1], vt[g // HALF_GROUPS])
+
+            for c in chunks_at(p, 0):
+                e_tiles[c] = attn_exp(c)
+            for c in chunks_at(p, 5):
+                attn_transpose(c, a_tiles[c])
+            for c in chunks_at(p, 3):
+                a_new = attn.tile([P, 2, 2, 4, 4, I], BF16, name="a_n")
+                a_tiles[c] = a_new
+                attn_scale(e_tiles[c], rec_tiles[c], a_tiles[c], 0)
+            for c in chunks_at(p, 4):
+                attn_scale(e_tiles[c], rec_tiles[c], a_tiles[c], 1)
+            for c in chunks_at(p, 1):
+                sum_tiles[c] = attn_sum(e_tiles[c])
+
+            for y in range(2):
+                if p == attn_ready(y):
+                    quantise_attn(y)
             for o in range(O):
                 for y in range(2):
                     if p == finish_period(o, y):

@@ -25,8 +25,9 @@ HALF_GROUPS = HEAD_GROUPS // 2
 N_HALVES = 2 * O
 W_AHEAD = 4
 MX_LAG = 2
-A_STARTS = [0, 0, 1, 4] + [HALF_GROUPS * n for n in (3, 4, 5, 6)]
 V_LAG = HALF_GROUPS + MX_LAG + 1
+A_SECOND = 3 * HALF_GROUPS
+A_PIECES = 4
 
 FLOPS = 2 * ROWS * O * FS * FS + 2 * B * O * LQ * I * LS * D
 
@@ -48,7 +49,7 @@ def tile_localcrossattention_pa_kernel(tc, scores, final_encoder_out, WV_w, WV_b
         w_bf = ctx.enter_context(tc.tile_pool(name="w_bf", bufs=2))
         w_mx = ctx.enter_context(tc.tile_pool(name="w_mx", bufs=MX_LAG + 2))
         work = ctx.enter_context(tc.tile_pool(name="work", bufs=2))
-        attn = ctx.enter_context(tc.tile_pool(name="attn", bufs=4))
+        attn = ctx.enter_context(tc.tile_pool(name="attn", bufs=1))
         psum = ctx.enter_context(tc.psum_pool(name="psum", bufs=8))
 
         ctx.enter_context(tc.manual_schedule())
@@ -93,9 +94,8 @@ def tile_localcrossattention_pa_kernel(tc, scores, final_encoder_out, WV_w, WV_b
             nc.sync.dma_start(out=w_raw[:], in_=w_groups[g // 8, g // 4 % 2, g % 4])
             return w_raw
 
-        def load_scores(s):
-            y, h = divmod(s, 4)
-            nc.sync.dma_start(out=s_raw[h:P:4, y], in_=score_rows[y, h])
+        def load_scores(y, h, part):
+            nc.sync.dma_start(out=s_raw[h:P:4, y, part], in_=score_rows[y, h][:, part])
 
         def transpose_w(p, w_raw):
             w_grp = w_bf.tile([P, 2, PASSES, P, 4], BF16, name="w_grp", align_bytes=64)
@@ -108,7 +108,7 @@ def tile_localcrossattention_pa_kernel(tc, scores, final_encoder_out, WV_w, WV_b
                         2 * half,
                         grp_words[:, w, 2 * half : 2 * half + 2, :, :],
                         perm_w[:],
-                        on_scalar=not (w == 1 and half == 1 and p < N_GROUPS - 2 and not chunks_at(p, 0)),
+                        on_scalar=not (w == 1 and half == 1 and vector_takes_a_bank(p)),
                     )
             return w_grp
 
@@ -159,51 +159,48 @@ def tile_localcrossattention_pa_kernel(tc, scores, final_encoder_out, WV_w, WV_b
                 in_=v_grp[:, rng].rearrange("p a x -> p (a x)"),
             )
 
-        def attn_exp(c):
-            y, qp = divmod(c, 4)
-            e_t = attn.tile([P, 2 * 4, I, 8], F32, name="e_t")
+        def attn_exp(y, e_y, part, lh):
             nc.scalar.activation(
-                out=e_t[:],
-                in_=s_raw[:, y, :, 64 * qp : 64 * qp + 64].rearrange("p i (m k) -> p m i k", k=8),
+                out=e_y[:, 16 * lh : 16 * lh + 16, part],
+                in_=s_raw[:, y, part, 128 * lh : 128 * lh + 128].rearrange("p i (m k) -> p m i k", k=8),
                 func=ACT.Exp,
             )
-            return e_t
 
-        def attn_sum(e_t):
-            ssum = attn.tile([P, 2, I], F32, name="ssum")
+        def attn_sum(e_y, ssum, part, lh):
             nc.vector.tensor_reduce(
-                out=ssum[:], in_=e_t[:].rearrange("p (l g) i k -> p l i g k", l=2), axis=AXIS.XY, op=ALU.add
+                out=ssum[:, 4 * lh : 4 * lh + 4, part],
+                in_=e_y[:, 16 * lh : 16 * lh + 16, part].rearrange("p (l g) i k -> p l i g k", g=4),
+                axis=AXIS.XY,
+                op=ALU.add,
             )
-            return ssum
 
         def attn_eps(ssum):
-            denom = attn.tile([P, 2, I], F32, name="denom")
+            denom = attn.tile([P, 8, I], F32, name="denom")
             nc.vector.tensor_scalar_add(out=denom[:], in0=ssum[:], scalar1=EPS)
             return denom
 
         def attn_reciprocal(denom):
-            small = attn.tile([P, 2, I], F32, name="small")
+            small = attn.tile([P, 8, I], F32, name="small")
             nc.vector.reciprocal(out=small[:], in_=denom[:])
             return small
 
         def attn_repeat(small):
-            rec = attn.tile([P, 2, 4 * I], F32, name="rec")
+            rec = attn.tile([P, 8, 4 * I], F32, name="rec")
             nc.vector.tensor_copy(
                 out=rec[:].rearrange("p l (g i) -> p l g i", g=4),
-                in_=small[:].unsqueeze(2).to_broadcast([P, 2, 4, I]),
+                in_=small[:].unsqueeze(2).to_broadcast([P, 8, 4, I]),
             )
             return rec
 
-        def attn_scale(e_t, rec, a_n, l):
+        def attn_scale(e_y, rec, a_n, l):
             nc.vector.tensor_tensor(
-                out=a_n[:, l].rearrange("p u q g i -> p q (g i) u"),
-                in0=e_t[:, 4 * l : 4 * l + 4].rearrange("p g i (q u) -> p q (g i) u", u=2),
+                out=a_n[:, l % 2].rearrange("p u q g i -> p q (g i) u"),
+                in0=e_y[:, 4 * l : 4 * l + 4].rearrange("p g i (q u) -> p q (g i) u", u=2),
                 in1=rec[:, l, :].unsqueeze(1).unsqueeze(3).to_broadcast([P, 4, 4 * I, 2]),
                 op=ALU.mult,
             )
 
-        def attn_transpose(c, a_n):
-            y, qp = divmod(c, 4)
+        def attn_transpose(y, qp, a_n):
             bank = psum.tile([P, 4, P], F32, name="a_bank", tag="bank")
             for l in range(2):
                 for u in range(2):
@@ -265,22 +262,23 @@ def tile_localcrossattention_pa_kernel(tc, scores, final_encoder_out, WV_w, WV_b
         a_tiles = {}
         v_tiles = {}
         results = {}
+        halves = (slice(0, I // 2), slice(I // 2, I))
+        enc_raw = const.tile([P, 2, FS], BF16)
+        bias_raw = const.tile([P, 4 * P], BF16)
+        for part in halves:
+            for h in range(4):
+                load_scores(0, h, part)
         w_new = w_in.tile([P, 2, FS], BF16, name="w_raw")
         for w in range(2):
             nc.sync.dma_start(out=w_new[:, w, :], in_=w_groups[0, 0, 0][:, w, :])
         w_raw[0] = w_new
-        enc_raw = const.tile([P, 2, FS], BF16)
         nc.sync.dma_start(out=enc_raw[:], in_=enc_rows)
-        bias_raw = const.tile([P, 4 * P], BF16)
         nc.vector.memset(bias_raw[:], 0.0)
         nc.sync.dma_start(out=bias_raw[0 : O * HALF_GROUPS, :], in_=bias_rows)
-        for s in range(4):
-            load_scores(s)
-        w_raw[1] = load_w(1)
-        w_raw[2] = load_w(2)
-        w_raw[3] = load_w(3)
+        for g in range(1, W_AHEAD):
+            w_raw[g] = load_w(g)
 
-        def prepare_enc_and_bias():
+        def prepare_enc():
             enc_grp = const.tile([P, PASSES, ROWS, 4], BF16, align_bytes=64)
             raw_words = enc_raw[:].bitcast(F32)
             grp_words = enc_grp[:].bitcast(F32)
@@ -293,11 +291,24 @@ def tile_localcrossattention_pa_kernel(tc, scores, final_encoder_out, WV_w, WV_b
                         ident_f32[:],
                         on_scalar=(half == 0),
                     )
+            return enc_grp
+
+        def quantise_enc(enc_grp):
+            nc.vector.quantize_mx(
+                out=enc_codes[:].rearrange("p c r -> p (c r)").bitcast(FP8X4),
+                scales=enc_scales[:].rearrange("p c r -> p (c r)"),
+                in_=enc_grp[:].rearrange("p c r t -> p (c r t)"),
+            )
+
+        def prepare_bias():
             bias_ord = const.tile([P, 2, P], F32)
             nc.vector.tensor_copy(
                 out=bias_ord[:].rearrange("p h (q y u) -> p h q y u", q=4, u=2),
                 in_=bias_raw[:].bitcast(F32).rearrange("p (q u y h) -> p h q y u", q=4, u=2, h=2),
             )
+            return bias_ord
+
+        def place_bias(bias_ord):
             bias_bank = psum.tile([P, 2, P], F32, name="bias_bank", tag="bank")
             for h in range(2):
                 nc.tensor.transpose(bias_bank[:, h, :], bias_ord[:, h, :], ident_f32[:])
@@ -305,51 +316,77 @@ def tile_localcrossattention_pa_kernel(tc, scores, final_encoder_out, WV_w, WV_b
                 out=bias_sb[:],
                 in_=bias_bank[:].bitcast(BF16).rearrange("p h (r w) -> p r h w", w=2)[:, 0 : O * HALF_GROUPS],
             )
-            nc.vector.quantize_mx(
-                out=enc_codes[:].rearrange("p c r -> p (c r)").bitcast(FP8X4),
-                scales=enc_scales[:].rearrange("p c r -> p (c r)"),
-                in_=enc_grp[:].rearrange("p c r t -> p (c r t)"),
-            )
 
-        def chunks_at(p, offset):
-            return [c for c, start in enumerate(A_STARTS) if start == p - offset]
+        def exp_period(k):
+            return A_SECOND + 2 * k
+
+        def reciprocal_period(y):
+            return 0 if y == 0 else exp_period(A_PIECES)
+
+        def scale_period(y, qp):
+            return reciprocal_period(y) + 1 + (qp if y == 0 else 2 * qp)
+
+        def turn_period(y, qp):
+            return scale_period(y, qp + 1)
 
         def attn_ready(y):
-            return A_STARTS[4 * y + 3] + 6
+            return turn_period(y, 3) + 1
 
         def finish_period(o, y):
             return max(HALF_GROUPS * (2 * o + 1) + V_LAG + 3 + y, attn_ready(y) + 1 + o)
+
+        def vector_takes_a_bank(p):
+            scaling = any(p == scale_period(y, qp) for y in range(2) for qp in range(4))
+            return 1 <= p < N_GROUPS - 1 and not scaling
+
+        def new_exponentials(y):
+            e_new = attn.tile([P, 8 * 4, I, 8], F32, name="e_y")
+            s_new = attn.tile([P, 8, I], F32, name="ssum")
+            e_tiles[y] = e_new
+            sum_tiles[y] = s_new
+
+        new_exponentials(0)
+        for k in range(A_PIECES):
+            attn_exp(0, e_tiles[0], halves[k // 2], k % 2)
+        for k in range(A_PIECES):
+            attn_sum(e_tiles[0], sum_tiles[0], halves[k // 2], k % 2)
 
         for p in range(finish_period(O - 1, 1) + 1):
             if 0 <= p < N_GROUPS - W_AHEAD:
                 w_raw[p + W_AHEAD] = load_w(p + W_AHEAD)
             if 4 <= p < 4 + 4:
-                load_scores(p - 4 + 4)
+                load_scores(1, p - 4, slice(0, I))
 
             if 1 <= p <= N_GROUPS:
                 w_quant[p - 1] = quantise_w(w_grp[p - 1], p == N_GROUPS)
-
-            for c in chunks_at(p, 2):
-                den_tiles[c] = attn_eps(sum_tiles[c])
-            for c in chunks_at(p, 3):
-                rec_tiles[c] = attn_repeat(small_tiles[c])
+            for y in range(2):
+                if p == reciprocal_period(y) + 1:
+                    rec_tiles[y] = attn_repeat(small_tiles[y])
 
             if 0 <= p < N_GROUPS:
                 w_grp[p] = transpose_w(p, w_raw[p])
+            if p == 1:
+                place_bias(bias_ord)
+            for y in range(2):
+                if p == reciprocal_period(y):
+                    den_tiles[y] = attn_eps(sum_tiles[y])
             if p == 0:
-                prepare_enc_and_bias()
-            for c in chunks_at(p, 2):
-                small_tiles[c] = attn_reciprocal(den_tiles[c])
+                bias_ord = prepare_bias()
+
             hh, piece = divmod(p - V_LAG, HALF_GROUPS)
             if 0 <= hh < N_HALVES and piece < 2:
                 if piece == 0:
                     v_new = work.tile([P, 4, 4 * 2 * 4 * 16], BF16, name="v_grp", align_bytes=64)
                     v_tiles[hh] = v_new
                 transpose_values(piece, vt[hh], v_tiles[hh])
-
+            for y in range(2):
+                if p == reciprocal_period(y):
+                    small_tiles[y] = attn_reciprocal(den_tiles[y])
             hh, piece = divmod(p - 1 - V_LAG, HALF_GROUPS)
             if 0 <= hh < N_HALVES and piece < 2:
                 quantise_values(hh // 2, hh % 2, piece, v_tiles[hh])
+            if p == 0:
+                quantise_enc(prepare_enc())
 
             g = p - MX_LAG
             if 0 <= g < N_GROUPS:
@@ -358,18 +395,25 @@ def tile_localcrossattention_pa_kernel(tc, scores, final_encoder_out, WV_w, WV_b
                     vt[g // HALF_GROUPS] = vt_new
                 project(g, w_quant[g][0], w_quant[g][1], vt[g // HALF_GROUPS])
 
-            for c in chunks_at(p, 0):
-                e_tiles[c] = attn_exp(c)
-            for c in chunks_at(p, 5):
-                attn_transpose(c, a_tiles[c])
-            for c in chunks_at(p, 3):
-                a_new = attn.tile([P, 2, 2, 4, 4, I], BF16, name="a_n")
-                a_tiles[c] = a_new
-                attn_scale(e_tiles[c], rec_tiles[c], a_tiles[c], 0)
-            for c in chunks_at(p, 4):
-                attn_scale(e_tiles[c], rec_tiles[c], a_tiles[c], 1)
-            for c in chunks_at(p, 1):
-                sum_tiles[c] = attn_sum(e_tiles[c])
+            for k in range(A_PIECES):
+                if p == exp_period(k):
+                    if k == 0:
+                        new_exponentials(1)
+                    attn_exp(1, e_tiles[1], halves[k // 2], k % 2)
+            for y in range(2):
+                for qp in range(4):
+                    if p == turn_period(y, qp):
+                        attn_transpose(y, qp, a_tiles[y, qp])
+            for y in range(2):
+                for qp in range(4):
+                    if p == scale_period(y, qp):
+                        a_new = attn.tile([P, 2, 2, 4, 4, I], BF16, name="a_n", bufs=3)
+                        a_tiles[y, qp] = a_new
+                        for l in range(2):
+                            attn_scale(e_tiles[y], rec_tiles[y], a_new, 2 * qp + l)
+            for k in range(A_PIECES):
+                if p == exp_period(k) + 1:
+                    attn_sum(e_tiles[1], sum_tiles[1], halves[k // 2], k % 2)
 
             for y in range(2):
                 if p == attn_ready(y):

@@ -46,7 +46,7 @@ def tile_localcrossattention_pa_kernel(tc, scores, final_encoder_out, WV_w, WV_b
     with ExitStack() as ctx:
         const = ctx.enter_context(tc.tile_pool(name="const", bufs=1))
         w_in = ctx.enter_context(tc.tile_pool(name="w_in", bufs=W_AHEAD + 2))
-        w_bf = ctx.enter_context(tc.tile_pool(name="w_bf", bufs=2))
+        w_bf = ctx.enter_context(tc.tile_pool(name="w_bf", bufs=3))
         w_mx = ctx.enter_context(tc.tile_pool(name="w_mx", bufs=MX_LAG + 2))
         work = ctx.enter_context(tc.tile_pool(name="work", bufs=2))
         attn = ctx.enter_context(tc.tile_pool(name="attn", bufs=1))
@@ -54,6 +54,10 @@ def tile_localcrossattention_pa_kernel(tc, scores, final_encoder_out, WV_w, WV_b
 
         ctx.enter_context(tc.manual_schedule())
 
+        zero = const.tile([P, 1], F32)
+        nc.vector.memset(zero[:], 0.0)
+        one = const.tile([P, 1], F32)
+        nc.scalar.activation(out=one[:], in_=zero[:], func=ACT.Exp)
         ident_f32 = const.tile([P, P], F32)
         make_identity(nc, ident_f32[:])
         perm_w = const.tile([P, P], F32)
@@ -242,7 +246,7 @@ def tile_localcrossattention_pa_kernel(tc, scores, final_encoder_out, WV_w, WV_b
             for gl in range(2):
                 dst = o_sb[:, o, 2 * y + gl].rearrange("p b (y m) -> p b y m", m=4)
                 src = res[:, gl].rearrange("p m b y -> p b y m")
-                if gl == 0:
+                if y == 1:
                     nc.scalar.mul(out=dst, in_=src, mul=COEFF)
                 else:
                     nc.vector.tensor_scalar(out=dst, in0=src, scalar1=COEFF, scalar2=None, op0=ALU.mult)
@@ -263,7 +267,6 @@ def tile_localcrossattention_pa_kernel(tc, scores, final_encoder_out, WV_w, WV_b
         v_tiles = {}
         results = {}
         halves = (slice(0, I // 2), slice(I // 2, I))
-        enc_raw = const.tile([P, 2, FS], BF16)
         bias_raw = const.tile([P, 4 * P], BF16)
         for part in halves:
             for h in range(4):
@@ -272,6 +275,7 @@ def tile_localcrossattention_pa_kernel(tc, scores, final_encoder_out, WV_w, WV_b
         for w in range(2):
             nc.sync.dma_start(out=w_new[:, w, :], in_=w_groups[0, 0, 0][:, w, :])
         w_raw[0] = w_new
+        enc_raw = w_in.tile([P, 2, FS], BF16, name="enc_raw", tag="w_raw")
         nc.sync.dma_start(out=enc_raw[:], in_=enc_rows)
         nc.vector.memset(bias_raw[:], 0.0)
         nc.sync.dma_start(out=bias_raw[0 : O * HALF_GROUPS, :], in_=bias_rows)
@@ -279,7 +283,7 @@ def tile_localcrossattention_pa_kernel(tc, scores, final_encoder_out, WV_w, WV_b
             w_raw[g] = load_w(g)
 
         def prepare_enc():
-            enc_grp = const.tile([P, PASSES, ROWS, 4], BF16, align_bytes=64)
+            enc_grp = w_bf.tile([P, PASSES, ROWS, 4], BF16, name="enc_grp", tag="w_grp", align_bytes=64)
             raw_words = enc_raw[:].bitcast(F32)
             grp_words = enc_grp[:].bitcast(F32)
             for h in range(2):
@@ -357,7 +361,7 @@ def tile_localcrossattention_pa_kernel(tc, scores, final_encoder_out, WV_w, WV_b
             if 4 <= p < 4 + 4:
                 load_scores(1, p - 4, slice(0, I))
 
-            if 1 <= p <= N_GROUPS:
+            if 2 <= p <= N_GROUPS:
                 w_quant[p - 1] = quantise_w(w_grp[p - 1], p == N_GROUPS)
             for y in range(2):
                 if p == reciprocal_period(y) + 1:
@@ -386,6 +390,7 @@ def tile_localcrossattention_pa_kernel(tc, scores, final_encoder_out, WV_w, WV_b
             if 0 <= hh < N_HALVES and piece < 2:
                 quantise_values(hh // 2, hh % 2, piece, v_tiles[hh])
             if p == 0:
+                w_quant[0] = quantise_w(w_grp[0], False)
                 quantise_enc(prepare_enc())
 
             g = p - MX_LAG

@@ -243,13 +243,12 @@ def tile_localcrossattention_pa_kernel(tc, scores, final_encoder_out, WV_w, WV_b
             return res
 
         def finish_copies(o, y, res):
-            for gl in range(2):
-                dst = o_sb[:, o, 2 * y + gl].rearrange("p b (y m) -> p b y m", m=4)
-                src = res[:, gl].rearrange("p m b y -> p b y m")
-                if y == 1:
-                    nc.scalar.mul(out=dst, in_=src, mul=COEFF)
-                else:
-                    nc.vector.tensor_scalar(out=dst, in0=src, scalar1=COEFF, scalar2=None, op0=ALU.mult)
+            dst = o_sb[:, o, 2 * y : 2 * y + 2].rearrange("p g b (y m) -> p g b y m", m=4)
+            src = res[:].rearrange("p g m b y -> p g b y m")
+            if y == 1:
+                nc.scalar.mul(out=dst, in_=src, mul=COEFF)
+            else:
+                nc.vector.tensor_scalar(out=dst, in0=src, scalar1=COEFF, scalar2=None, op0=ALU.mult)
             if y == 1:
                 for b4 in range(4):
                     nc.sync.dma_start(out=out_rows[o, b4], in_=o_sb[32 * b4 : 32 * b4 + 32, o, :, b4, :])
@@ -337,7 +336,7 @@ def tile_localcrossattention_pa_kernel(tc, scores, final_encoder_out, WV_w, WV_b
             return turn_period(y, 3) + 1
 
         def finish_period(o, y):
-            return max(HALF_GROUPS * (2 * o + 1) + V_LAG + 3 + y, attn_ready(y) + 1 + o)
+            return max(HALF_GROUPS * (2 * o + 1) + V_LAG + 3 + y, attn_ready(y) + 1 + o + (o > 0))
 
         def vector_takes_a_bank(p):
             scaling = any(p == scale_period(y, qp) for y in range(2) for qp in range(4))

from contextlib import ExitStack

import concourse.mybir as mybir
from concourse.masks import make_identity

BF16 = mybir.dt.bfloat16
F32 = mybir.dt.float32
U32 = mybir.dt.uint32
U8 = mybir.dt.uint8
FP8X4 = mybir.dt.float8_e4m3fn_x4
ACT = mybir.ActivationFunctionType
ALU = mybir.AluOpType
AXIS = mybir.AxisListType

P = 128
B, O, I, LQ, LS, D = 16, 4, 16, 32, 32, 64
FS = LS * D
EPS = 1e-5
COEFF = 0.125
PASSES = FS // 512
ROWS = B * I
N_GROUPS = O * FS // (2 * P)
HEAD_GROUPS = N_GROUPS // O
HALF_GROUPS = HEAD_GROUPS // 2
N_HALVES = 2 * O
W_AHEAD = 4
MX_LAG = 2
V_LAG = HALF_GROUPS + MX_LAG + 1
A_SECOND = 3 * HALF_GROUPS
A_PIECES = 4

FLOPS = 2 * ROWS * O * FS * FS + 2 * B * O * LQ * I * LS * D


def tile_localcrossattention_pa_kernel(tc, scores, final_encoder_out, WV_w, WV_b, out):
    nc = tc.nc

    w_groups = WV_w.rearrange("o (g p h w) f -> o h g p w f", p=P, h=2, w=2)
    enc_rows = final_encoder_out.rearrange("b (i s) d -> (b i) (s d)", i=I).rearrange(
        "(h r) f -> r h f", h=2
    )
    score_rows = scores.rearrange("(y b) o i (h l) k -> y h (b o) i (l k)", y=2, h=4)
    bias_rows = WV_b.rearrange("o (g x) -> (o g) x", x=4 * P)
    out_rows = out.rearrange("(g b) (o q) d -> o b q g d", b=4, o=O)

    with ExitStack() as ctx:
        const = ctx.enter_context(tc.tile_pool(name="const", bufs=1))
        w_in = ctx.enter_context(tc.tile_pool(name="w_in", bufs=W_AHEAD + 2))
        w_bf = ctx.enter_context(tc.tile_pool(name="w_bf", bufs=3))
        w_mx = ctx.enter_context(tc.tile_pool(name="w_mx", bufs=MX_LAG + 2))
        work = ctx.enter_context(tc.tile_pool(name="work", bufs=2))
        attn = ctx.enter_context(tc.tile_pool(name="attn", bufs=1))
        psum = ctx.enter_context(tc.psum_pool(name="psum", bufs=8))

        ctx.enter_context(tc.manual_schedule())

        zero = const.tile([P, 1], F32)
        nc.vector.memset(zero[:], 0.0)
        one = const.tile([P, 1], F32)
        nc.scalar.activation(out=one[:], in_=zero[:], func=ACT.Exp)
        ident_f32 = const.tile([P, P], F32)
        make_identity(nc, ident_f32[:])
        perm_w = const.tile([P, P], F32)
        nc.vector.tensor_copy(
            out=perm_w[:].rearrange("p (q y u) -> p q y u", q=4, u=2),
            in_=ident_f32[:].rearrange("p (q u y) -> p q y u", q=4, u=2),
        )
        perm_a = const.tile([P, P], F32)
        nc.vector.tensor_copy(
            out=perm_a[:].rearrange("p (o b h) -> p o b h", o=O, b=8),
            in_=ident_f32[:].rearrange("p (b o h) -> p o b h", b=8, o=O),
        )

        enc_codes = const.tile([P, PASSES, ROWS], U32, align_bytes=64)
        enc_scales = const.tile([P, PASSES, ROWS], U8, align_bytes=64)
        bias_sb = const.tile([P, O * HALF_GROUPS, 2, 2], F32)
        s_raw = const.tile([P, 2, I, 8 * LS], BF16)
        a_grp = const.tile([P, 2, 32, 4, 4, 2, 2, 2], BF16, align_bytes=64)
        a_codes = const.tile([P, 2, 32, LQ], U32, align_bytes=64)
        a_scales = const.tile([P, 2, 32, LQ], U8, align_bytes=64)
        v_codes = const.tile([P, O, 2, 4, 2 * 4 * 16], U32, align_bytes=64)
        v_scales = const.tile([P, O, 2, 4, 2 * 4 * 16], U8, align_bytes=64)
        o_sb = const.tile([P, O, 4, 4, D], F32)

        def transpose_two_passes(words, first_pass, grouped_words, perm, on_scalar):
            bank = psum.tile([P, 2, 2, P], F32, name="bank", tag="bank")
            for c in range(2):
                for u in range(2):
                    blk = 2 * (first_pass + c) + u
                    nc.tensor.transpose(bank[:, c, u, :], words[:, blk * P : (blk + 1) * P], perm)
            if on_scalar:
                nc.scalar.copy(out=grouped_words, in_=bank[:].rearrange("p c u n -> p c n u"))
            else:
                nc.vector.tensor_copy(out=grouped_words, in_=bank[:].rearrange("p c u n -> p c n u"))

        def load_w(g):
            w_raw = w_in.tile([P, 2, FS], BF16, name="w_raw")
            nc.sync.dma_start(out=w_raw[:], in_=w_groups[g // 8, g // 4 % 2, g % 4])
            return w_raw

        def load_scores(y, h, part):
            nc.sync.dma_start(out=s_raw[h:P:4, y, part], in_=score_rows[y, h][:, part])

        def transpose_w(p, w_raw):
            w_grp = w_bf.tile([P, 2, PASSES, P, 4], BF16, name="w_grp", align_bytes=64)
            raw_words = w_raw[:].bitcast(F32)
            grp_words = w_grp[:].bitcast(F32)
            for w in range(2):
                for half in range(2):
                    transpose_two_passes(
                        raw_words[:, w, :],
                        2 * half,
                        grp_words[:, w, 2 * half : 2 * half + 2, :, :],
                        perm_w[:],
                        on_scalar=not (w == 1 and half == 1 and vector_takes_a_bank(p)),
                    )
            return w_grp

        def quantise_w(w_grp, last):
            w_codes = w_mx.tile([P, 2, PASSES, P], U32, name="w_codes", align_bytes=64)
            w_scales = w_mx.tile([P, 2, PASSES, P], U8, name="w_scales", align_bytes=64)
            for part in (slice(0, 1), slice(1, 2)) if last else (slice(0, 2),):
                nc.vector.quantize_mx(
                    out=w_codes[:, part].rearrange("p w c n -> p (w c n)").bitcast(FP8X4),
                    scales=w_scales[:, part].rearrange("p w c n -> p (w c n)"),
                    in_=w_grp[:, part].rearrange("p w c n t -> p (w c n t)"),
                )
            return w_codes, w_scales

        def project(g, w_codes, w_scales, vt):
            acc = psum.tile([P, 2, ROWS], F32, name="acc", tag="bank")
            for w in range(2):
                for c in range(PASSES):
                    nc.tensor.matmul_mx(
                        out=acc[:, w, :],
                        lhsT=w_codes[:, w, c, :].bitcast(FP8X4),
                        lhsT_scale=w_scales[:, w, c, :],
                        rhs=enc_codes[:, c, :].bitcast(FP8X4),
                        rhs_scale=enc_scales[:, c, :],
                        start=(c == 0),
                        stop=(c == PASSES - 1),
                    )
            for w in range(2):
                nc.scalar.activation(
                    out=vt[:, :, w, :, g % 4, :],
                    in_=acc[:, w, :].rearrange("p (a b i) -> p a b i", a=4, i=I),
                    func=ACT.Identity,
                    bias=bias_sb[:, 4 * (g // HEAD_GROUPS) + g % 4, g // 4 % 2, w : w + 1],
                    scale=1.0,
                )

        def transpose_values(half, vt, v_grp):
            nc.vector.transpose(
                out=v_grp[:, 2 * half : 2 * half + 2].rearrange("p a x -> p (a x)").bitcast(F32),
                in_=vt[:, 2 * half : 2 * half + 2].rearrange("p a w b g i -> p (a w b g i)").bitcast(F32),
            )

        def quantise_values(o, h, half, v_grp):
            rng = slice(2 * half, 2 * half + 2)
            nc.vector.quantize_mx(
                out=v_codes[:, o, h, rng, :].rearrange("p a n -> p (a n)").bitcast(FP8X4),
                scales=v_scales[:, o, h, rng, :].rearrange("p a n -> p (a n)"),
                in_=v_grp[:, rng].rearrange("p a x -> p (a x)"),
            )

        def attn_exp(y, e_y, part, lh):
            nc.scalar.activation(
                out=e_y[:, 16 * lh : 16 * lh + 16, part],
                in_=s_raw[:, y, part, 128 * lh : 128 * lh + 128].rearrange("p i (m k) -> p m i k", k=8),
                func=ACT.Exp,
            )

        def attn_sum(e_y, ssum, part, lh):
            nc.vector.tensor_reduce(
                out=ssum[:, 4 * lh : 4 * lh + 4, part],
                in_=e_y[:, 16 * lh : 16 * lh + 16, part].rearrange("p (l g) i k -> p l i g k", g=4),
                axis=AXIS.XY,
                op=ALU.add,
            )

        def attn_eps(ssum):
            denom = attn.tile([P, 8, I], F32, name="denom")
            nc.vector.tensor_scalar_add(out=denom[:], in0=ssum[:], scalar1=EPS)
            return denom

        def attn_reciprocal(denom):
            small = attn.tile([P, 8, I], F32, name="small")
            nc.vector.reciprocal(out=small[:], in_=denom[:])
            return small

        def attn_repeat(small):
            rec = attn.tile([P, 8, 4 * I], F32, name="rec")
            nc.vector.tensor_copy(
                out=rec[:].rearrange("p l (g i) -> p l g i", g=4),
                in_=small[:].unsqueeze(2).to_broadcast([P, 8, 4, I]),
            )
            return rec

        def attn_scale(e_y, rec, a_n, l):
            nc.vector.tensor_tensor(
                out=a_n[:, l % 2].rearrange("p u q g i -> p q (g i) u"),
                in0=e_y[:, 4 * l : 4 * l + 4].rearrange("p g i (q u) -> p q (g i) u", u=2),
                in1=rec[:, l, :].unsqueeze(1).unsqueeze(3).to_broadcast([P, 4, 4 * I, 2]),
                op=ALU.mult,
            )

        def attn_transpose(y, qp, a_n):
            bank = psum.tile([P, 4, P], F32, name="a_bank", tag="bank")
            for l in range(2):
                for u in range(2):
                    nc.tensor.transpose(
                        bank[:, 2 * l + u, :],
                        a_n[:, l, u].rearrange("p q g i -> p (q g i)").bitcast(F32),
                        perm_a[:],
                    )
            nc.scalar.copy(
                out=a_grp[:, y].rearrange("p x h r l u e -> p x h r (l u e)").bitcast(F32)[:, :, :, qp, :],
                in_=bank[:].rearrange("p s (x h) -> p x h s", h=4),
            )

        def quantise_attn(y):
            nc.vector.quantize_mx(
                out=a_codes[:, y].rearrange("p x q -> p (x q)").bitcast(FP8X4),
                scales=a_scales[:, y].rearrange("p x q -> p (x q)"),
                in_=a_grp[:, y].rearrange("p x h r l u e -> p (x h r l u e)"),
            )

        def finish_passes(o, y):
            res = psum.tile([P, 2, 4, 4, 16], F32, name="res", tag="bank")
            for gl in range(2):
                a = 2 * y + gl
                x0 = 8 * o + 4 * gl
                for h in range(2):
                    nc.tensor.matmul_mx(
                        out=res[:, gl, 2 * h : 2 * h + 2].rearrange("p w b y -> p (w b y)"),
                        lhsT=a_codes[:, y, x0 : x0 + 4, :].rearrange("p x q -> p (x q)").bitcast(FP8X4),
                        lhsT_scale=a_scales[:, y, x0 : x0 + 4, :].rearrange("p x q -> p (x q)"),
                        rhs=v_codes[:, o, h, a, :].bitcast(FP8X4),
                        rhs_scale=v_scales[:, o, h, a, :],
                        start=True,
                        stop=True,
                    )
            return res

        def finish_copies(o, y, res):
            dst = o_sb[:, o, 2 * y : 2 * y + 2].rearrange("p g b (y m) -> p g b y m", m=4)
            src = res[:].rearrange("p g m b y -> p g b y m")
            if y == 1:
                nc.scalar.mul(out=dst, in_=src, mul=COEFF)
            else:
                nc.vector.tensor_scalar(out=dst, in0=src, scalar1=COEFF, scalar2=None, op0=ALU.mult)
            if y == 1:
                for b4 in range(4):
                    nc.sync.dma_start(out=out_rows[o, b4], in_=o_sb[32 * b4 : 32 * b4 + 32, o, :, b4, :])

        w_raw = {}
        w_grp = {}
        w_quant = {}
        vt = {}
        e_tiles = {}
        sum_tiles = {}
        den_tiles = {}
        small_tiles = {}
        rec_tiles = {}
        a_tiles = {}
        v_tiles = {}
        results = {}
        halves = (slice(0, I // 2), slice(I // 2, I))
        bias_raw = const.tile([P, 4 * P], BF16)
        for part in halves:
            for h in range(4):
                load_scores(0, h, part)
        w_new = w_in.tile([P, 2, FS], BF16, name="w_raw")
        for w in range(2):
            nc.sync.dma_start(out=w_new[:, w, :], in_=w_groups[0, 0, 0][:, w, :])
        w_raw[0] = w_new
        enc_raw = w_in.tile([P, 2, FS], BF16, name="enc_raw", tag="w_raw")
        nc.sync.dma_start(out=enc_raw[:], in_=enc_rows)
        nc.vector.memset(bias_raw[:], 0.0)
        nc.sync.dma_start(out=bias_raw[0 : O * HALF_GROUPS, :], in_=bias_rows)
        for g in range(1, W_AHEAD):
            w_raw[g] = load_w(g)

        def prepare_enc():
            enc_grp = w_bf.tile([P, PASSES, ROWS, 4], BF16, name="enc_grp", tag="w_grp", align_bytes=64)
            raw_words = enc_raw[:].bitcast(F32)
            grp_words = enc_grp[:].bitcast(F32)
            for h in range(2):
                for half in range(2):
                    transpose_two_passes(
                        raw_words[:, h, :],
                        2 * half,
                        grp_words[:, 2 * half : 2 * half + 2, P * h : P * (h + 1), :],
                        ident_f32[:],
                        on_scalar=(half == 0),
                    )
            return enc_grp

        def quantise_enc(enc_grp):
            nc.vector.quantize_mx(
                out=enc_codes[:].rearrange("p c r -> p (c r)").bitcast(FP8X4),
                scales=enc_scales[:].rearrange("p c r -> p (c r)"),
                in_=enc_grp[:].rearrange("p c r t -> p (c r t)"),
            )

        def prepare_bias():
            bias_ord = const.tile([P, 2, P], F32)
            nc.vector.tensor_copy(
                out=bias_ord[:].rearrange("p h (q y u) -> p h q y u", q=4, u=2),
                in_=bias_raw[:].bitcast(F32).rearrange("p (q u y h) -> p h q y u", q=4, u=2, h=2),
            )
            return bias_ord

        def place_bias(bias_ord):
            bias_bank = psum.tile([P, 2, P], F32, name="bias_bank", tag="bank")
            for h in range(2):
                nc.tensor.transpose(bias_bank[:, h, :], bias_ord[:, h, :], ident_f32[:])
            nc.vector.tensor_copy(
                out=bias_sb[:],
                in_=bias_bank[:].bitcast(BF16).rearrange("p h (r w) -> p r h w", w=2)[:, 0 : O * HALF_GROUPS],
            )

        def exp_period(k):
            return A_SECOND + 2 * k

        def reciprocal_period(y):
            return 0 if y == 0 else exp_period(A_PIECES)

        def scale_period(y, qp):
            return reciprocal_period(y) + 1 + (qp if y == 0 else 2 * qp)

        def turn_period(y, qp):
            return scale_period(y, qp + 1)

        def attn_ready(y):
            return turn_period(y, 3) + 1

        def finish_period(o, y):
            return max(HALF_GROUPS * (2 * o + 1) + V_LAG + 3 + y, attn_ready(y) + 1 + o + (o > 0))

        def vector_takes_a_bank(p):
            scaling = any(p == scale_period(y, qp) for y in range(2) for qp in range(4))
            return 1 <= p < N_GROUPS - 1 and not scaling

        def new_exponentials(y):
            e_new = attn.tile([P, 8 * 4, I, 8], F32, name="e_y")
            s_new = attn.tile([P, 8, I], F32, name="ssum")
            e_tiles[y] = e_new
            sum_tiles[y] = s_new

        new_exponentials(0)
        for k in range(A_PIECES):
            attn_exp(0, e_tiles[0], halves[k // 2], k % 2)
        for k in range(A_PIECES):
            attn_sum(e_tiles[0], sum_tiles[0], halves[k // 2], k % 2)

        for p in range(finish_period(O - 1, 1) + 1):
            if 0 <= p < N_GROUPS - W_AHEAD:
                w_raw[p + W_AHEAD] = load_w(p + W_AHEAD)
            if 4 <= p < 4 + 4:
                load_scores(1, p - 4, slice(0, I))

            if 2 <= p <= N_GROUPS:
                w_quant[p - 1] = quantise_w(w_grp[p - 1], p == N_GROUPS)
            for y in range(2):
                if p == reciprocal_period(y) + 1:
                    rec_tiles[y] = attn_repeat(small_tiles[y])

            if 0 <= p < N_GROUPS:
                w_grp[p] = transpose_w(p, w_raw[p])
            if p == 1:
                place_bias(bias_ord)
            for y in range(2):
                if p == reciprocal_period(y):
                    den_tiles[y] = attn_eps(sum_tiles[y])
            if p == 0:
                bias_ord = prepare_bias()

            hh, piece = divmod(p - V_LAG, HALF_GROUPS)
            if 0 <= hh < N_HALVES and piece < 2:
                if piece == 0:
                    v_new = work.tile([P, 4, 4 * 2 * 4 * 16], BF16, name="v_grp", align_bytes=64)
                    v_tiles[hh] = v_new
                transpose_values(piece, vt[hh], v_tiles[hh])
            for y in range(2):
                if p == reciprocal_period(y):
                    small_tiles[y] = attn_reciprocal(den_tiles[y])
            hh, piece = divmod(p - 1 - V_LAG, HALF_GROUPS)
            if 0 <= hh < N_HALVES and piece < 2:
                quantise_values(hh // 2, hh % 2, piece, v_tiles[hh])
            if p == 0:
                w_quant[0] = quantise_w(w_grp[0], False)
                quantise_enc(prepare_enc())

            g = p - MX_LAG
            if 0 <= g < N_GROUPS:
                if g % HALF_GROUPS == 0:
                    vt_new = work.tile([P, 4, 2, 4, 4, I], BF16, name="vt", align_bytes=64)
                    vt[g // HALF_GROUPS] = vt_new
                project(g, w_quant[g][0], w_quant[g][1], vt[g // HALF_GROUPS])

            for k in range(A_PIECES):
                if p == exp_period(k):
                    if k == 0:
                        new_exponentials(1)
                    attn_exp(1, e_tiles[1], halves[k // 2], k % 2)
            for y in range(2):
                for qp in range(4):
                    if p == turn_period(y, qp):
                        attn_transpose(y, qp, a_tiles[y, qp])
            for y in range(2):
                for qp in range(4):
                    if p == scale_period(y, qp):
                        a_new = attn.tile([P, 2, 2, 4, 4, I], BF16, name="a_n", bufs=3)
                        a_tiles[y, qp] = a_new
                        for l in range(2):
                            attn_scale(e_tiles[y], rec_tiles[y], a_new, 2 * qp + l)
            for k in range(A_PIECES):
                if p == exp_period(k) + 1:
                    attn_sum(e_tiles[1], sum_tiles[1], halves[k // 2], k % 2)

            for y in range(2):
                if p == attn_ready(y):
                    quantise_attn(y)
            for o in range(O):
                for y in range(2):
                    if p == finish_period(o, y):
                        results[o, y] = finish_passes(o, y)
                        finish_copies(o, y, results[o, y])
